import numpy as np
import ml_dtypes


def mxq(x, axis, fmt="e4m3"):
    dtype, down = {"e4m3": (ml_dtypes.float8_e4m3fn, 7), "e5m2": (ml_dtypes.float8_e5m2, 14)}[fmt]
    v = np.moveaxis(np.asarray(x, np.float32).astype(ml_dtypes.bfloat16).astype(np.float64), axis, -1)
    blocks = v.reshape(v.shape[:-1] + (-1, 32))
    amax = np.abs(blocks).max(-1, keepdims=True)
    byte = np.maximum(np.where(amax > 0, np.frexp(amax)[1] - 1 + 127, 0) - down, 1)
    scale = np.exp2(byte - 127.0)
    codes = (blocks / scale).astype(np.float32).astype(dtype).astype(np.float64)
    return np.moveaxis((codes * scale).reshape(v.shape), -1, axis)


WIDE = False


def mx_kscale(k):
    if not WIDE:
        return np.ones(k)
    levels = np.array([10, -10, 5, -5, 0])
    if k % 512:
        return np.exp2(np.random.permutation(np.resize(levels, k // 32))).repeat(32)
    a = np.empty((k // 512, 16))
    for p in range(k // 512):
        a[p, :8] = np.random.permutation(np.resize(levels, 8))
        for g in range(8):
            far = levels[np.abs(levels - a[p, g]) >= 10]
            a[p, g + 8] = far[np.random.randint(len(far))]
    return np.exp2(a.ravel()).repeat(32)


BF16 = ml_dtypes.bfloat16


def bf(x):
    return np.asarray(x, np.float32).astype(BF16)


def f64(x):
    return np.asarray(x).astype(np.float64)


B, S, DM, H, KV, HD = 2, 256, 2048, 16, 4, 128
THETA = 10000.0
EPS = 1e-6
HALF = HD // 2


def rmsnorm(u, gain):
    var = np.mean(np.square(u), axis=-1, keepdims=True)
    return (u * (1.0 / np.sqrt(var + EPS))) * gain


def rope(u):
    timescale = THETA ** (2.0 * np.arange(HALF) / HD)
    ang = np.arange(S)[:, None] / timescale[None, :]
    sin, cos = np.sin(ang)[None, :, None, :], np.cos(ang)[None, :, None, :]
    u1, u2 = u[..., :HALF], u[..., HALF:]
    return np.concatenate([u1 * cos - u2 * sin, u2 * cos + u1 * sin], axis=-1)


def draw0():
    s = mx_kscale(DM)
    w = 1.0 / np.sqrt(DM)
    return {"x": bf(np.random.standard_normal((B, S, DM)) * s),
            "wq": bf(np.random.standard_normal((DM, H, HD)) * w / s[:, None, None]),
            "wk": bf(np.random.standard_normal((DM, KV, HD)) * w / s[:, None, None]),
            "wv": bf(np.random.standard_normal((DM, KV, HD)) * w / s[:, None, None]),
            "q_scale": bf(1.0 + 0.1 * np.random.standard_normal(HD)),
            "k_scale": bf(1.0 + 0.1 * np.random.standard_normal(HD))}


def core(x, wq, wk, wv, q_scale, k_scale):
    xq = mxq(f64(x).reshape(B * S, DM), 1, "e4m3")
    q = (xq @ mxq(f64(wq).reshape(DM, H * HD), 0, "e4m3")).reshape(B, S, H, HD)
    k = (xq @ mxq(f64(wk).reshape(DM, KV * HD), 0, "e4m3")).reshape(B, S, KV, HD)
    v = (xq @ mxq(f64(wv).reshape(DM, KV * HD), 0, "e4m3")).reshape(B, S, KV, HD)
    q = rope(rmsnorm(q, f64(q_scale)))
    k = rope(rmsnorm(k, f64(k_scale)))
    return q, k, v


def e4m3fn_bytes(y):
    return np.clip(np.asarray(y, np.float64), -448.0, 448.0).astype(np.float32).astype(ml_dtypes.float8_e4m3fn).view(np.uint8)


def e4m3fn_values(b):
    return np.asarray(b, np.uint8).view(ml_dtypes.float8_e4m3fn).astype(np.float64)


def setup_inputs():
    d = draw0()
    x0 = np.asarray(d['wq']).astype(np.float64)
    s = (np.max(np.abs(x0), axis=(1, 2), keepdims=True) / 448.0).astype(np.float32)
    out = {}
    for k, v in d.items():
        if k == 'wq':
            out['wq_bytes'] = e4m3fn_bytes(x0 / s.astype(np.float64))
            out['wq_scale'] = s
        else:
            out[k] = v
    return out


def reference(x, wq_bytes, wq_scale, wk, wv, q_scale, k_scale):
    return core(x, e4m3fn_values(wq_bytes) * wq_scale.astype(np.float64), wk, wv, q_scale, k_scale)

@@ -1,0 +1,318 @@
+from contextlib import ExitStack
+
+import concourse.mybir as mybir
+from concourse.masks import make_identity
+
+F32 = mybir.dt.float32
+BF16 = mybir.dt.bfloat16
+U32 = mybir.dt.uint32
+I32 = mybir.dt.int32
+U8 = mybir.dt.uint8
+FP8 = mybir.dt.float8_e4m3fn
+FP8X4 = mybir.dt.float8_e4m3fn_x4
+ACT = mybir.ActivationFunctionType
+ALU = mybir.AluOpType
+
+P = 128
+PACK = 4
+DM = 2048
+PASSES = 4
+TOKENS = 512
+MT = 4
+NT = 512
+HD = 128
+HALF = 64
+HEADS_PER_TILE = 4
+THETA = 10000.0
+EPS = 1e-6
+PI = 3.141592653589793
+TWO_PI_HI = 6.28125
+TWO_PI_LO = 2.0 * PI - TWO_PI_HI
+
+FLOPS = 2 * TOKENS * DM * (2048 + 512 + 512)
+
+TILES = (("k", 0), ("q", 0), ("q", 1), ("q", 2), ("q", 3), ("v", 0))
+UNITS = len(TILES) * PASSES
+WIDEN_LEAD = 4
+EPI_LAG = 6
+SCALAR_INTERLEAVES = (17, 19, 20, 21, 23)
+MANUAL = False
+
+
+def tile_attention_pa_kernel(tc, x, wq_bytes, wq_scale, wk, wv, q_scale, k_scale, out_0, out_1, out_2):
+    nc = tc.nc
+    x_flat = x.flatten_outer_dims()
+    wqb_v = wq_bytes.rearrange("(g p t) h d -> g p t (h d)", p=P, t=PACK)
+    wqs_v = wq_scale.rearrange("(g p t) a b -> p g (t a b)", p=P, t=PACK)
+    wk_v = wk.rearrange("(g p t) h d -> g p t (h d)", p=P, t=PACK)
+    wv_v = wv.rearrange("(g p t) h d -> g p t (h d)", p=P, t=PACK)
+    dst = {
+        "q": out_0.rearrange("b s h d -> (b s) (h d)"),
+        "k": out_1.rearrange("b s h d -> (b s) (h d)"),
+        "v": out_2.rearrange("b s h d -> (b s) (h d)"),
+    }
+
+    with ExitStack() as ctx:
+        const = ctx.enter_context(tc.tile_pool(name="const", bufs=1))
+        raw = ctx.enter_context(tc.tile_pool(name="raw", bufs=1))
+        keep = ctx.enter_context(tc.tile_pool(name="keep", bufs=1))
+        work = ctx.enter_context(tc.tile_pool(name="work", bufs=3))
+        psum = ctx.enter_context(tc.psum_pool(name="psum", bufs=8))
+        if MANUAL:
+            ctx.enter_context(tc.manual_schedule())
+
+        scl = const.tile([P, PASSES, PACK], F32, name="wq_scales")
+        nc.sync.dma_start(out=scl[:], in_=wqs_v)
+        x_raw = [raw.tile([P, DM], BF16, name="x_raw%d" % m) for m in range(MT)]
+        wq_b = {}
+        w_raw = {}
+        for j in range(4):
+            for g in range(PASSES):
+                wq_b[(j, g)] = raw.tile([P, PACK, NT], U8, name="wq_bytes_%d_%d" % (j, g))
+        for kind in ("k", "v"):
+            for g in range(PASSES):
+                w_raw[(kind, g)] = raw.tile([P, PACK, NT], BF16, name="w%s_raw%d" % (kind, g))
+        gain = {"q": const.tile([P, HD], BF16, name="gain_q"), "k": const.tile([P, HD], BF16, name="gain_k")}
+
+        def load_wq(j, g):
+            nc.sync.dma_start(out=wq_b[(j, g)][:], in_=wqb_v[g][:, :, j * NT : (j + 1) * NT])
+
+        for g in range(PASSES):
+            load_wq(0, g)
+            nc.sync.dma_start(out=w_raw[("k", g)][:], in_=wk_v[g])
+            nc.sync.dma_start(out=x_raw[g][:], in_=x_flat[g * P : (g + 1) * P, :])
+        nc.sync.dma_start(out=gain["q"][:], in_=q_scale.partition_broadcast(P))
+        nc.sync.dma_start(out=gain["k"][:], in_=k_scale.partition_broadcast(P))
+        for j in range(1, 4):
+            for g in range(PASSES):
+                load_wq(j, g)
+        for g in range(PASSES):
+            nc.sync.dma_start(out=w_raw[("v", g)][:], in_=wv_v[g])
+
+        ident = const.tile([P, P], F32, name="ident")
+        make_identity(nc, ident[:])
+
+        pos_i = const.tile([P, 2], I32, name="pos_i")
+        nc.gpsimd.iota(pos_i[:], pattern=[[P, 2]], base=0, channel_multiplier=1)
+        pos = const.tile([P, 2], F32, name="pos")
+        nc.vector.tensor_copy(out=pos[:], in_=pos_i[:])
+        freq = const.tile([P, HALF], F32, name="freq")
+        nc.vector.memset(freq[:, 0:1], 1.0)
+        for b in range(6):
+            w = 1 << b
+            nc.vector.tensor_scalar(out=freq[:, w : 2 * w], in0=freq[:, 0:w], scalar1=pow(THETA, -w / 64.0), scalar2=None, op0=ALU.mult)
+        arg = const.tile([P, 2, 2, HALF], F32, name="arg")
+        for j in range(2):
+            nc.vector.tensor_scalar(out=arg[:, 0, j, :], in0=freq[:], scalar1=pos[:, j : j + 1], scalar2=None, op0=ALU.mult)
+            nc.vector.tensor_scalar(out=arg[:, 1, j, :], in0=freq[:], scalar1=pos[:, j : j + 1], scalar2=PI / 2.0, op0=ALU.mult, op1=ALU.add)
+        argf = arg[:].rearrange("p a j i -> p (a j i)")
+        turns_i = const.tile([P, 4 * HALF], I32, name="turns_i")
+        nc.vector.tensor_scalar(out=turns_i[:], in0=argf, scalar1=1.0 / (2.0 * PI), scalar2=None, op0=ALU.mult)
+        turns = const.tile([P, 4 * HALF], F32, name="turns")
+        nc.vector.tensor_copy(out=turns[:], in_=turns_i[:])
+        red1 = const.tile([P, 4 * HALF], F32, name="red1")
+        nc.vector.scalar_tensor_tensor(out=red1[:], in0=turns[:], scalar=-TWO_PI_HI, in1=argf, op0=ALU.mult, op1=ALU.add)
+        red2 = const.tile([P, 4 * HALF], F32, name="red2")
+        nc.vector.scalar_tensor_tensor(out=red2[:], in0=turns[:], scalar=-TWO_PI_LO, in1=red1[:], op0=ALU.mult, op1=ALU.add)
+        over = const.tile([P, 4 * HALF], F32, name="over")
+        nc.vector.tensor_scalar(out=over[:], in0=red2[:], scalar1=PI, scalar2=None, op0=ALU.is_gt)
+        red3 = const.tile([P, 4 * HALF], F32, name="red3")
+        nc.vector.scalar_tensor_tensor(out=red3[:], in0=over[:], scalar=-TWO_PI_HI, in1=red2[:], op0=ALU.mult, op1=ALU.add)
+        red4 = const.tile([P, 4 * HALF], F32, name="red4")
+        nc.vector.scalar_tensor_tensor(out=red4[:], in0=over[:], scalar=-TWO_PI_LO, in1=red3[:], op0=ALU.mult, op1=ALU.add)
+        trig = const.tile([P, 2, 2, HALF], F32, name="trig")
+        nc.scalar.activation(out=trig[:].rearrange("p a j i -> p (a j i)"), in_=red4[:], func=ACT.Sin)
+
+        tab_a = {}
+        tab_b = {}
+
+        def build_tables():
+            for kind in ("k", "q"):
+                g = gain[kind]
+                for j in range(2):
+                    sin_j = trig[:, 0, j, :]
+                    cos_j = trig[:, 1, j, :]
+                    a = const.tile([P, HD], F32, name="tab_a_%s%d" % (kind, j))
+                    b = const.tile([P, HD], F32, name="tab_b_%s%d" % (kind, j))
+                    nc.vector.tensor_tensor(out=a[:, 0:HALF], in0=g[:, 0:HALF], in1=cos_j, op=ALU.mult)
+                    nc.vector.tensor_tensor(out=a[:, HALF:HD], in0=g[:, HALF:HD], in1=cos_j, op=ALU.mult)
+                    nc.vector.scalar_tensor_tensor(out=b[:, 0:HALF], in0=g[:, HALF:HD], scalar=-1.0, in1=sin_j, op0=ALU.mult, op1=ALU.mult)
+                    nc.vector.tensor_tensor(out=b[:, HALF:HD], in0=g[:, 0:HALF], in1=sin_j, op=ALU.mult)
+                    tab_a[(kind, j)] = a
+                    tab_b[(kind, j)] = b
+
+        x_codes = [keep.tile([P, PASSES * P], U32, name="x_codes%d" % m, align_bytes=64) for m in range(MT)]
+        x_scales = [keep.tile([P, PASSES * P], U8, name="x_scales%d" % m, align_bytes=64) for m in range(MT)]
+        x_grp = {}
+
+        def x_turn(m):
+            words = x_raw[m][:].bitcast(F32)
+            grp = work.tile([P, PASSES, P, PACK], BF16, name="x_grp", bufs=2, align_bytes=64)
+            x_grp[m] = grp
+            grp_words = grp[:].rearrange("p g r t -> p (g r t)").bitcast(F32).rearrange("p (g r u) -> p g r u", g=PASSES, u=2)
+            for gp in range(2):
+                xt = psum.tile([P, 2, 2, P], F32, name="bank")
+                for g2 in range(2):
+                    g = 2 * gp + g2
+                    for u in range(2):
+                        nc.tensor.transpose(xt[:, g2, u, :], words[:, 256 * g + u : 256 * (g + 1) : 2], ident[:])
+                src = xt[:].rearrange("p g u r -> p g r u")
+                if gp == 0:
+                    nc.vector.tensor_copy(out=grp_words[:, 0:2], in_=src)
+                else:
+                    nc.scalar.copy(out=grp_words[:, 2:4], in_=src)
+
+        def x_quant(m):
+            nc.vector.quantize_mx(
+                out=x_codes[m][:].bitcast(FP8X4), scales=x_scales[m][:], in_=x_grp[m][:].rearrange("p g r t -> p (g r t)")
+            )
+
+        wide = {}
+        grouped = {}
+        w_codes = {}
+        w_scales = {}
+
+        def widen(u):
+            kind, j = TILES[u // PASSES]
+            g = u % PASSES
+            wd = work.tile([P, PACK, NT], BF16, name="wide", bufs=5)
+            wide[u] = wd
+            for t in range(PACK):
+                nc.scalar.activation(out=wd[:, t, :], in_=wq_b[(j, g)][:, t, :].bitcast(FP8), func=ACT.Copy, scale=scl[:, g, t : t + 1])
+
+        def interleave(u):
+            kind, j = TILES[u // PASSES]
+            src = wide[u] if kind == "q" else w_raw[(kind, u % PASSES)]
+            grp = work.tile([P, NT, PACK], BF16, name="grouped", bufs=3, align_bytes=64)
+            grouped[u] = grp
+            if u in SCALAR_INTERLEAVES:
+                nc.scalar.copy(out=grp[:], in_=src[:].rearrange("p t n -> p n t"))
+            else:
+                nc.vector.tensor_copy(out=grp[:], in_=src[:].rearrange("p t n -> p n t"))
+
+        def quantise(u):
+            w_codes[u] = work.tile([P, NT], U32, name="w_codes", bufs=6, align_bytes=64)
+            w_scales[u] = work.tile([P, NT], U8, name="w_scales", bufs=6, align_bytes=64)
+            nc.vector.quantize_mx(out=w_codes[u][:].bitcast(FP8X4), scales=w_scales[u][:], in_=grouped[u][:].rearrange("p n t -> p (n t)"))
+
+        acc = {}
+
+        def multiply(u):
+            ti = u // PASSES
+            g = u % PASSES
+            for m in range(MT):
+                if g == 0:
+                    acc[(ti, m)] = psum.tile([P, NT], F32, name="bank")
+                nc.tensor.matmul_mx(
+                    out=acc[(ti, m)][:],
+                    lhsT=x_codes[m][:, g * P : (g + 1) * P].bitcast(FP8X4),
+                    lhsT_scale=x_scales[m][:, g * P : (g + 1) * P],
+                    rhs=w_codes[u][:].bitcast(FP8X4),
+                    rhs_scale=w_scales[u][:],
+                    start=(g == 0),
+                    stop=(g == PASSES - 1),
+                )
+
+        rstd = {}
+        rooted = {}
+        prod1 = {}
+        prod2 = {}
+        summed = {}
+
+        def squares(ti, m):
+            ss = work.tile([P, HEADS_PER_TILE], F32, name="sumsq", bufs=3)
+            for h in range(HEADS_PER_TILE):
+                junk = work.tile([P, HD], BF16, name="junk", bufs=2)
+                nc.scalar.activation(out=junk[:], in_=acc[(ti, m)][:, h * HD : (h + 1) * HD], func=ACT.Square, accum_out=ss[:, h : h + 1])
+            rt = work.tile([P, HEADS_PER_TILE], F32, name="rooted", bufs=3)
+            nc.scalar.activation(out=rt[:], in_=ss[:], func=ACT.Sqrt, bias=EPS, scale=1.0 / HD)
+            rooted[(ti, m)] = rt
+
+        def recip(ti, m):
+            r = work.tile([P, HEADS_PER_TILE], F32, name="rstd", bufs=3)
+            nc.vector.reciprocal(out=r[:], in_=rooted[(ti, m)][:])
+            rstd[(ti, m)] = r
+
+        def rope_mul(ti, m):
+            kind = TILES[ti][0]
+            a = tab_a[(kind, m % 2)]
+            b = tab_b[(kind, m % 2)]
+            u3 = acc[(ti, m)][:].rearrange("p (h d) -> p h d", h=HEADS_PER_TILE)
+            u4 = acc[(ti, m)][:].rearrange("p (h c i) -> p h c i", h=HEADS_PER_TILE, c=2)
+            t1 = work.tile([P, HEADS_PER_TILE, HD], F32, name="prod1", bufs=2)
+            t2 = work.tile([P, HEADS_PER_TILE, 2, HALF], F32, name="prod2", bufs=2)
+            nc.vector.tensor_tensor(out=t1[:], in0=u3, in1=a[:].unsqueeze(1).to_broadcast([P, HEADS_PER_TILE, HD]), op=ALU.mult)
+            nc.vector.tensor_tensor(
+                out=t2[:, :, 0, :], in0=u4[:, :, 1, :], in1=b[:, 0:HALF].unsqueeze(1).to_broadcast([P, HEADS_PER_TILE, HALF]), op=ALU.mult
+            )
+            nc.vector.tensor_tensor(
+                out=t2[:, :, 1, :], in0=u4[:, :, 0, :], in1=b[:, HALF:HD].unsqueeze(1).to_broadcast([P, HEADS_PER_TILE, HALF]), op=ALU.mult
+            )
+            prod1[(ti, m)] = t1
+            prod2[(ti, m)] = t2
+
+        def rope_add(ti, m):
+            sm = work.tile([P, NT], F32, name="summed", bufs=3)
+            nc.vector.tensor_tensor(
+                out=sm[:], in0=prod1[(ti, m)][:].rearrange("p h d -> p (h d)"), in1=prod2[(ti, m)][:].rearrange("p h c i -> p (h c i)"), op=ALU.add
+            )
+            summed[(ti, m)] = sm
+
+        def finish(ti, m):
+            kind, j = TILES[ti]
+            y = work.tile([P, NT], F32, name="result", bufs=4)
+            for h in range(HEADS_PER_TILE):
+                nc.scalar.activation(
+                    out=y[:, h * HD : (h + 1) * HD], in_=summed[(ti, m)][:, h * HD : (h + 1) * HD], func=ACT.Copy, scale=rstd[(ti, m)][:, h : h + 1]
+                )
+            nc.sync.dma_start(out=dst[kind][m * P : (m + 1) * P, j * NT : (j + 1) * NT], in_=y[:])
+
+        def v_out(ti, m):
+            y = work.tile([P, NT], F32, name="result", bufs=4)
+            if m % 2 == 0:
+                nc.vector.tensor_copy(out=y[:], in_=acc[(ti, m)][:])
+            else:
+                nc.scalar.copy(out=y[:], in_=acc[(ti, m)][:])
+            nc.sync.dma_start(out=dst["v"][m * P : (m + 1) * P, :], in_=y[:])
+
+        def epi_bank(s):
+            e = s - EPI_LAG
+            if e < 0 or e >= UNITS:
+                return None
+            ti, m = e // MT, e % MT
+            return (ti, m) if TILES[ti][0] != "v" else None
+
+        for s in range(UNITS + EPI_LAG + 2):
+            e = epi_bank(s)
+            e_prev = epi_bank(s - 1)
+            if s == 4:
+                build_tables()
+            if e is not None:
+                squares(e[0], e[1])
+            uw = s + WIDEN_LEAD
+            if uw < UNITS and TILES[uw // PASSES][0] == "q":
+                widen(uw)
+            if e_prev is not None:
+                finish(e_prev[0], e_prev[1])
+            if e is not None:
+                rope_mul(e[0], e[1])
+            if s < MT:
+                x_turn(s)
+            if 1 <= s <= UNITS:
+                quantise(s - 1)
+            if e is not None:
+                rope_add(e[0], e[1])
+            if s < UNITS:
+                interleave(s)
+            if s < MT:
+                x_quant(s)
+            if e is not None:
+                recip(e[0], e[1])
+            if s == MT:
+                for u in range(0, MT):
+                    multiply(u)
+            elif MT < s <= UNITS:
+                multiply(s - 1)
+            if s == UNITS + 1:
+                for m in range(MT):
+                    v_out(len(TILES) - 1, m)

@@ -33,10 +33,10 @@ FLOPS = 2 * TOKENS * DM * (2048 + 512 + 512)
 
 TILES = (("k", 0), ("q", 0), ("q", 1), ("q", 2), ("q", 3), ("v", 0))
 UNITS = len(TILES) * PASSES
-WIDEN_LEAD = 4
-EPI_LAG = 6
-SCALAR_INTERLEAVES = (17, 19, 20, 21, 23)
-MANUAL = False
+SEQ = "TR13 WD4 TR2 TR2 IV0 WD5 TR2 QU0 IV1 WD6 IV4 XP0 QU1 WD7 XV0.0 QU4 IV2 XS0.1 IV5 XP1 WD8 XQ0 XV1.0 XS1.1 QU2 WD9 IV3 XP2 XQ1 QU3 WD10 XV2.0 QU5 XP3 IV6 XS2.1 XS3.1 XV3.0 SN XQ2 WD11 XQ3 TB MM0 MM1 WD12 QU6 IV7 MM2 IV8 MM3 WD13 MM4 QU7 QU8 MM5 IV9 SQ0.0 SQ0.1 MM6 RC0.0 RM0.0 SQ0.2 MM7 SQ0.3 RM0.1 AG0.0 WD14 RM0.2 AG0.1 RM0.3 AG0.2 FN0.0 RC0.1 WD15 RC0.2 MM8 RC0.3 AV0.3 QU9 IV10 MM9 FN0.1 FN0.2 IV11 FN0.3 SQ1.0 QU10 QU11 SQ1.1 MM10 RC1.0 RM1.0 SQ1.2 MM11 SQ1.3 RM1.1 AG1.0 WD16 RM1.2 AG1.1 RM1.3 AG1.2 WD17 RC1.1 RC1.2 RC1.3 AV1.3 IV12 FN1.0 FN1.1 IV13 FN1.2 WD18 QU12 QU13 MM12 IV14 MM13 FN1.3 IV15 WD19 QU14 QU15 MM14 SQ2.0 IV16 SQ2.1 MM15 RC2.0 SQ2.2 RM2.0 SQ2.3 RM2.1 AG2.0 SQ3.0 RM2.2 SQ3.1 AG2.1 FN2.0 RM2.3 SQ3.2 AG2.2 SQ3.3 RC2.1 RC2.2 RC2.3 AV2.3 FN2.1 QU16 FN2.2 IV17 MM16 FN2.3 IS20 IV18 QU17 QU18 MM17 IS21 RC3.0 RC3.1 RC3.2 RC3.3 IV19 MM18 RM3.0 RM3.1 AG3.0 RM3.2 AG3.1 FN3.0 RM3.3 AG3.2 FN3.1 QU19 FN3.2 AV3.3 MM19 QU20 FN3.3 QU21 MM20 IS23 IV22 MM21 QU22 SQ4.0 QU23 MM22 SQ4.1 RC4.0 RM4.0 MM23 SQ4.2 RM4.1 AG4.0 SQ4.3 OS1 RM4.2 AG4.1 FN4.0 OS3 RM4.3 AG4.2 RC4.1 RC4.2 RC4.3 FN4.1 AV4.3 FN4.2 OV0 FN4.3 OV2"
+DMA_ORDER = "q00 k0 q01 k1 q02 x0 q03 k2 q10 x1 q11 k3 q12 x2 q13 x3 g q20 q21 q22 q23 v0 q30 v1 q31 v2 q32 v3 q33"
+CFG = {"WIDE_BUFS": 6, "GRP_BUFS": 3, "CODE_BUFS": 8}
+MANUAL = True
 
 
 def tile_attention_pa_kernel(tc, x, wq_bytes, wq_scale, wk, wv, q_scale, k_scale, out_0, out_1, out_2):
@@ -77,51 +77,67 @@ def tile_attention_pa_kernel(tc, x, wq_bytes, wq_scale, wk, wv, q_scale, k_scale
         def load_wq(j, g):
             nc.sync.dma_start(out=wq_b[(j, g)][:], in_=wqb_v[g][:, :, j * NT : (j + 1) * NT])
 
-        for g in range(PASSES):
-            load_wq(0, g)
-            nc.sync.dma_start(out=w_raw[("k", g)][:], in_=wk_v[g])
-            nc.sync.dma_start(out=x_raw[g][:], in_=x_flat[g * P : (g + 1) * P, :])
-        nc.sync.dma_start(out=gain["q"][:], in_=q_scale.partition_broadcast(P))
-        nc.sync.dma_start(out=gain["k"][:], in_=k_scale.partition_broadcast(P))
-        for j in range(1, 4):
-            for g in range(PASSES):
-                load_wq(j, g)
-        for g in range(PASSES):
-            nc.sync.dma_start(out=w_raw[("v", g)][:], in_=wv_v[g])
+        for item in DMA_ORDER.split(" "):
+            kind0 = item[0]
+            if kind0 == "q":
+                load_wq(int(item[1]), int(item[2]))
+            elif kind0 == "k":
+                nc.sync.dma_start(out=w_raw[("k", int(item[1]))][:], in_=wk_v[int(item[1])])
+            elif kind0 == "v":
+                nc.sync.dma_start(out=w_raw[("v", int(item[1]))][:], in_=wv_v[int(item[1])])
+            elif kind0 == "x":
+                g = int(item[1])
+                nc.sync.dma_start(out=x_raw[g][:], in_=x_flat[g * P : (g + 1) * P, :])
+            else:
+                nc.sync.dma_start(out=gain["q"][:], in_=q_scale.partition_broadcast(P))
+                nc.sync.dma_start(out=gain["k"][:], in_=k_scale.partition_broadcast(P))
 
         ident = const.tile([P, P], F32, name="ident")
         make_identity(nc, ident[:])
 
+        zero1 = const.tile([P, 1], F32, name="zero1")
+        nc.vector.memset(zero1[:], 0.0)
+        warm = const.tile([P, 1], F32, name="warm")
+        nc.scalar.activation(out=warm[:], in_=zero1[:], func=ACT.Sin)
         pos_i = const.tile([P, 2], I32, name="pos_i")
         nc.gpsimd.iota(pos_i[:], pattern=[[P, 2]], base=0, channel_multiplier=1)
         pos = const.tile([P, 2], F32, name="pos")
-        nc.vector.tensor_copy(out=pos[:], in_=pos_i[:])
         freq = const.tile([P, HALF], F32, name="freq")
-        nc.vector.memset(freq[:, 0:1], 1.0)
-        for b in range(6):
-            w = 1 << b
-            nc.vector.tensor_scalar(out=freq[:, w : 2 * w], in0=freq[:, 0:w], scalar1=pow(THETA, -w / 64.0), scalar2=None, op0=ALU.mult)
         arg = const.tile([P, 2, 2, HALF], F32, name="arg")
-        for j in range(2):
-            nc.vector.tensor_scalar(out=arg[:, 0, j, :], in0=freq[:], scalar1=pos[:, j : j + 1], scalar2=None, op0=ALU.mult)
-            nc.vector.tensor_scalar(out=arg[:, 1, j, :], in0=freq[:], scalar1=pos[:, j : j + 1], scalar2=PI / 2.0, op0=ALU.mult, op1=ALU.add)
         argf = arg[:].rearrange("p a j i -> p (a j i)")
-        turns_i = const.tile([P, 4 * HALF], I32, name="turns_i")
-        nc.vector.tensor_scalar(out=turns_i[:], in0=argf, scalar1=1.0 / (2.0 * PI), scalar2=None, op0=ALU.mult)
-        turns = const.tile([P, 4 * HALF], F32, name="turns")
-        nc.vector.tensor_copy(out=turns[:], in_=turns_i[:])
-        red1 = const.tile([P, 4 * HALF], F32, name="red1")
-        nc.vector.scalar_tensor_tensor(out=red1[:], in0=turns[:], scalar=-TWO_PI_HI, in1=argf, op0=ALU.mult, op1=ALU.add)
-        red2 = const.tile([P, 4 * HALF], F32, name="red2")
-        nc.vector.scalar_tensor_tensor(out=red2[:], in0=turns[:], scalar=-TWO_PI_LO, in1=red1[:], op0=ALU.mult, op1=ALU.add)
-        over = const.tile([P, 4 * HALF], F32, name="over")
-        nc.vector.tensor_scalar(out=over[:], in0=red2[:], scalar1=PI, scalar2=None, op0=ALU.is_gt)
-        red3 = const.tile([P, 4 * HALF], F32, name="red3")
-        nc.vector.scalar_tensor_tensor(out=red3[:], in0=over[:], scalar=-TWO_PI_HI, in1=red2[:], op0=ALU.mult, op1=ALU.add)
-        red4 = const.tile([P, 4 * HALF], F32, name="red4")
-        nc.vector.scalar_tensor_tensor(out=red4[:], in0=over[:], scalar=-TWO_PI_LO, in1=red3[:], op0=ALU.mult, op1=ALU.add)
+        turns_i = work.tile([P, 4 * HALF], I32, name="trig_tmp", bufs=7)
+        turns = work.tile([P, 4 * HALF], F32, name="trig_tmp", bufs=7)
+        red1 = work.tile([P, 4 * HALF], F32, name="trig_tmp", bufs=7)
+        red2 = work.tile([P, 4 * HALF], F32, name="trig_tmp", bufs=7)
+        over = work.tile([P, 4 * HALF], F32, name="trig_tmp", bufs=7)
+        red3 = work.tile([P, 4 * HALF], F32, name="trig_tmp", bufs=7)
+        red4 = work.tile([P, 4 * HALF], F32, name="trig_tmp", bufs=7)
         trig = const.tile([P, 2, 2, HALF], F32, name="trig")
-        nc.scalar.activation(out=trig[:].rearrange("p a j i -> p (a j i)"), in_=red4[:], func=ACT.Sin)
+        trig_ops = []
+        trig_ops.append(lambda: nc.vector.memset(freq[:, 0:1], 1.0))
+        trig_ops.append(lambda: nc.vector.tensor_copy(out=pos[:], in_=pos_i[:]))
+        for b in range(6):
+            trig_ops.append(lambda w=(1 << b): nc.vector.tensor_scalar(out=freq[:, w : 2 * w], in0=freq[:, 0:w], scalar1=pow(THETA, -w / 64.0), scalar2=None, op0=ALU.mult))
+        for j in range(2):
+            trig_ops.append(lambda j=j: nc.vector.tensor_scalar(out=arg[:, 0, j, :], in0=freq[:], scalar1=pos[:, j : j + 1], scalar2=None, op0=ALU.mult))
+            trig_ops.append(lambda j=j: nc.vector.tensor_scalar(out=arg[:, 1, j, :], in0=freq[:], scalar1=pos[:, j : j + 1], scalar2=PI / 2.0, op0=ALU.mult, op1=ALU.add))
+        trig_ops.append(lambda: nc.vector.tensor_scalar(out=turns_i[:], in0=argf, scalar1=1.0 / (2.0 * PI), scalar2=None, op0=ALU.mult))
+        trig_ops.append(lambda: nc.vector.tensor_copy(out=turns[:], in_=turns_i[:]))
+        trig_ops.append(lambda: nc.vector.scalar_tensor_tensor(out=red1[:], in0=turns[:], scalar=-TWO_PI_HI, in1=argf, op0=ALU.mult, op1=ALU.add))
+        trig_ops.append(lambda: nc.vector.scalar_tensor_tensor(out=red2[:], in0=turns[:], scalar=-TWO_PI_LO, in1=red1[:], op0=ALU.mult, op1=ALU.add))
+        trig_ops.append(lambda: nc.vector.tensor_scalar(out=over[:], in0=red2[:], scalar1=PI, scalar2=None, op0=ALU.is_gt))
+        trig_ops.append(lambda: nc.vector.scalar_tensor_tensor(out=red3[:], in0=over[:], scalar=-TWO_PI_HI, in1=red2[:], op0=ALU.mult, op1=ALU.add))
+        trig_ops.append(lambda: nc.vector.scalar_tensor_tensor(out=red4[:], in0=over[:], scalar=-TWO_PI_LO, in1=red3[:], op0=ALU.mult, op1=ALU.add))
+
+        trig_done = [0]
+
+        def take_trig(n):
+            for i in range(trig_done[0], min(trig_done[0] + n, len(trig_ops))):
+                trig_ops[i]()
+            trig_done[0] = trig_done[0] + n
+
+        def sines():
+            nc.scalar.activation(out=trig[:].rearrange("p a j i -> p (a j i)"), in_=red4[:], func=ACT.Sin)
 
         tab_a = {}
         tab_b = {}
@@ -145,22 +161,27 @@ def tile_attention_pa_kernel(tc, x, wq_bytes, wq_scale, wk, wv, q_scale, k_scale
         x_scales = [keep.tile([P, PASSES * P], U8, name="x_scales%d" % m, align_bytes=64) for m in range(MT)]
         x_grp = {}
 
-        def x_turn(m):
+        x_bank = {}
+
+        def x_trans(m):
             words = x_raw[m][:].bitcast(F32)
-            grp = work.tile([P, PASSES, P, PACK], BF16, name="x_grp", bufs=2, align_bytes=64)
-            x_grp[m] = grp
-            grp_words = grp[:].rearrange("p g r t -> p (g r t)").bitcast(F32).rearrange("p (g r u) -> p g r u", g=PASSES, u=2)
             for gp in range(2):
                 xt = psum.tile([P, 2, 2, P], F32, name="bank")
+                x_bank[(m, gp)] = xt
                 for g2 in range(2):
                     g = 2 * gp + g2
                     for u in range(2):
                         nc.tensor.transpose(xt[:, g2, u, :], words[:, 256 * g + u : 256 * (g + 1) : 2], ident[:])
-                src = xt[:].rearrange("p g u r -> p g r u")
-                if gp == 0:
-                    nc.vector.tensor_copy(out=grp_words[:, 0:2], in_=src)
-                else:
-                    nc.scalar.copy(out=grp_words[:, 2:4], in_=src)
+
+        def x_evac(m, gp, on_scalar):
+            if m not in x_grp:
+                x_grp[m] = work.tile([P, PASSES, P, PACK], BF16, name="x_grp", bufs=2, align_bytes=64)
+            grp_words = x_grp[m][:].rearrange("p g r t -> p (g r t)").bitcast(F32).rearrange("p (g r u) -> p g r u", g=PASSES, u=2)
+            src = x_bank[(m, gp)][:].rearrange("p g u r -> p g r u")
+            if on_scalar:
+                nc.scalar.copy(out=grp_words[:, 2 * gp : 2 * gp + 2], in_=src)
+            else:
+                nc.vector.tensor_copy(out=grp_words[:, 2 * gp : 2 * gp + 2], in_=src)
 
         def x_quant(m):
             nc.vector.quantize_mx(
@@ -175,24 +196,24 @@ def tile_attention_pa_kernel(tc, x, wq_bytes, wq_scale, wk, wv, q_scale, k_scale
         def widen(u):
             kind, j = TILES[u // PASSES]
             g = u % PASSES
-            wd = work.tile([P, PACK, NT], BF16, name="wide", bufs=5)
+            wd = work.tile([P, PACK, NT], BF16, name="wide", bufs=CFG["WIDE_BUFS"])
             wide[u] = wd
             for t in range(PACK):
                 nc.scalar.activation(out=wd[:, t, :], in_=wq_b[(j, g)][:, t, :].bitcast(FP8), func=ACT.Copy, scale=scl[:, g, t : t + 1])
 
-        def interleave(u):
+        def interleave(u, on_scalar):
             kind, j = TILES[u // PASSES]
             src = wide[u] if kind == "q" else w_raw[(kind, u % PASSES)]
-            grp = work.tile([P, NT, PACK], BF16, name="grouped", bufs=3, align_bytes=64)
+            grp = work.tile([P, NT, PACK], BF16, name=("grouped_s" if on_scalar else "grouped"), bufs=(2 if on_scalar else CFG["GRP_BUFS"]), align_bytes=64)
             grouped[u] = grp
-            if u in SCALAR_INTERLEAVES:
+            if on_scalar:
                 nc.scalar.copy(out=grp[:], in_=src[:].rearrange("p t n -> p n t"))
             else:
                 nc.vector.tensor_copy(out=grp[:], in_=src[:].rearrange("p t n -> p n t"))
 
         def quantise(u):
-            w_codes[u] = work.tile([P, NT], U32, name="w_codes", bufs=6, align_bytes=64)
-            w_scales[u] = work.tile([P, NT], U8, name="w_scales", bufs=6, align_bytes=64)
+            w_codes[u] = work.tile([P, NT], U32, name="w_codes", bufs=CFG["CODE_BUFS"], align_bytes=64)
+            w_scales[u] = work.tile([P, NT], U8, name="w_scales", bufs=CFG["CODE_BUFS"], align_bytes=64)
             nc.vector.quantize_mx(out=w_codes[u][:].bitcast(FP8X4), scales=w_scales[u][:], in_=grouped[u][:].rearrange("p n t -> p (n t)"))
 
         acc = {}
@@ -220,16 +241,16 @@ def tile_attention_pa_kernel(tc, x, wq_bytes, wq_scale, wk, wv, q_scale, k_scale
         summed = {}
 
         def squares(ti, m):
-            ss = work.tile([P, HEADS_PER_TILE], F32, name="sumsq", bufs=3)
+            ss = work.tile([P, HEADS_PER_TILE], F32, name="sumsq", bufs=12)
             for h in range(HEADS_PER_TILE):
                 junk = work.tile([P, HD], BF16, name="junk", bufs=2)
                 nc.scalar.activation(out=junk[:], in_=acc[(ti, m)][:, h * HD : (h + 1) * HD], func=ACT.Square, accum_out=ss[:, h : h + 1])
-            rt = work.tile([P, HEADS_PER_TILE], F32, name="rooted", bufs=3)
+            rt = work.tile([P, HEADS_PER_TILE], F32, name="rooted", bufs=12)
             nc.scalar.activation(out=rt[:], in_=ss[:], func=ACT.Sqrt, bias=EPS, scale=1.0 / HD)
             rooted[(ti, m)] = rt
 
         def recip(ti, m):
-            r = work.tile([P, HEADS_PER_TILE], F32, name="rstd", bufs=3)
+            r = work.tile([P, HEADS_PER_TILE], F32, name="rstd", bufs=12)
             nc.vector.reciprocal(out=r[:], in_=rooted[(ti, m)][:])
             rstd[(ti, m)] = r
 
@@ -239,8 +260,8 @@ def tile_attention_pa_kernel(tc, x, wq_bytes, wq_scale, wk, wv, q_scale, k_scale
             b = tab_b[(kind, m % 2)]
             u3 = acc[(ti, m)][:].rearrange("p (h d) -> p h d", h=HEADS_PER_TILE)
             u4 = acc[(ti, m)][:].rearrange("p (h c i) -> p h c i", h=HEADS_PER_TILE, c=2)
-            t1 = work.tile([P, HEADS_PER_TILE, HD], F32, name="prod1", bufs=2)
-            t2 = work.tile([P, HEADS_PER_TILE, 2, HALF], F32, name="prod2", bufs=2)
+            t1 = work.tile([P, HEADS_PER_TILE, HD], F32, name="prod1", bufs=4)
+            t2 = work.tile([P, HEADS_PER_TILE, 2, HALF], F32, name="prod2", bufs=4)
             nc.vector.tensor_tensor(out=t1[:], in0=u3, in1=a[:].unsqueeze(1).to_broadcast([P, HEADS_PER_TILE, HD]), op=ALU.mult)
             nc.vector.tensor_tensor(
                 out=t2[:, :, 0, :], in0=u4[:, :, 1, :], in1=b[:, 0:HALF].unsqueeze(1).to_broadcast([P, HEADS_PER_TILE, HALF]), op=ALU.mult
@@ -251,9 +272,10 @@ def tile_attention_pa_kernel(tc, x, wq_bytes, wq_scale, wk, wv, q_scale, k_scale
             prod1[(ti, m)] = t1
             prod2[(ti, m)] = t2
 
-        def rope_add(ti, m):
-            sm = work.tile([P, NT], F32, name="summed", bufs=3)
-            nc.vector.tensor_tensor(
+        def rope_add(ti, m, on_pool):
+            sm = work.tile([P, NT], F32, name=("summed_g" if on_pool else "summed_v"), bufs=(4 if on_pool else 2))
+            eng = nc.gpsimd if on_pool else nc.vector
+            eng.tensor_tensor(
                 out=sm[:], in0=prod1[(ti, m)][:].rearrange("p h d -> p (h d)"), in1=prod2[(ti, m)][:].rearrange("p h c i -> p (h c i)"), op=ALU.add
             )
             summed[(ti, m)] = sm
@@ -267,52 +289,55 @@ def tile_attention_pa_kernel(tc, x, wq_bytes, wq_scale, wk, wv, q_scale, k_scale
                 )
             nc.sync.dma_start(out=dst[kind][m * P : (m + 1) * P, j * NT : (j + 1) * NT], in_=y[:])
 
-        def v_out(ti, m):
-            y = work.tile([P, NT], F32, name="result", bufs=4)
-            if m % 2 == 0:
+        def v_out(ti, m, on_vector):
+            y = work.tile([P, NT], F32, name=("summed_v" if on_vector else "result"), bufs=(2 if on_vector else 4))
+            if on_vector:
                 nc.vector.tensor_copy(out=y[:], in_=acc[(ti, m)][:])
             else:
                 nc.scalar.copy(out=y[:], in_=acc[(ti, m)][:])
             nc.sync.dma_start(out=dst["v"][m * P : (m + 1) * P, :], in_=y[:])
 
-        def epi_bank(s):
-            e = s - EPI_LAG
-            if e < 0 or e >= UNITS:
-                return None
-            ti, m = e // MT, e % MT
-            return (ti, m) if TILES[ti][0] != "v" else None
-
-        for s in range(UNITS + EPI_LAG + 2):
-            e = epi_bank(s)
-            e_prev = epi_bank(s - 1)
-            if s == 4:
+        for tok in SEQ.split(" "):
+            op, a = tok[0:2], [int(z) for z in tok[2:].split(".") if z != ""]
+            if op == "TR":
+                take_trig(a[0])
+            elif op == "SN":
+                sines()
+            elif op == "TB":
                 build_tables()
-            if e is not None:
-                squares(e[0], e[1])
-            uw = s + WIDEN_LEAD
-            if uw < UNITS and TILES[uw // PASSES][0] == "q":
-                widen(uw)
-            if e_prev is not None:
-                finish(e_prev[0], e_prev[1])
-            if e is not None:
-                rope_mul(e[0], e[1])
-            if s < MT:
-                x_turn(s)
-            if 1 <= s <= UNITS:
-                quantise(s - 1)
-            if e is not None:
-                rope_add(e[0], e[1])
-            if s < UNITS:
-                interleave(s)
-            if s < MT:
-                x_quant(s)
-            if e is not None:
-                recip(e[0], e[1])
-            if s == MT:
-                for u in range(0, MT):
-                    multiply(u)
-            elif MT < s <= UNITS:
-                multiply(s - 1)
-            if s == UNITS + 1:
-                for m in range(MT):
-                    v_out(len(TILES) - 1, m)
+            elif op == "WD":
+                widen(a[0])
+            elif op == "IV":
+                interleave(a[0], False)
+            elif op == "IS":
+                interleave(a[0], True)
+            elif op == "QU":
+                quantise(a[0])
+            elif op == "MM":
+                multiply(a[0])
+            elif op == "XP":
+                x_trans(a[0])
+            elif op == "XV":
+                x_evac(a[0], a[1], False)
+            elif op == "XS":
+                x_evac(a[0], a[1], True)
+            elif op == "XQ":
+                x_quant(a[0])
+            elif op == "SQ":
+                squares(a[0], a[1])
+            elif op == "RC":
+                recip(a[0], a[1])
+            elif op == "RM":
+                rope_mul(a[0], a[1])
+            elif op == "AV":
+                rope_add(a[0], a[1], False)
+            elif op == "AG":
+                rope_add(a[0], a[1], True)
+            elif op == "FN":
+                finish(a[0], a[1])
+            elif op == "OV":
+                v_out(len(TILES) - 1, a[0], True)
+            elif op == "OS":
+                v_out(len(TILES) - 1, a[0], False)
+            else:
+                raise ValueError(tok)

@@ -33,8 +33,8 @@ FLOPS = 2 * TOKENS * DM * (2048 + 512 + 512)
 
 TILES = (("k", 0), ("q", 0), ("q", 1), ("q", 2), ("q", 3), ("v", 0))
 UNITS = len(TILES) * PASSES
-SEQ = "TR13 WD4 TR2 TR2 IV0 WD5 TR2 QU0 IV1 WD6 IV4 XP0 QU1 WD7 XV0.0 QU4 IV2 XS0.1 IV5 XP1 WD8 XQ0 XV1.0 XS1.1 QU2 WD9 IV3 XP2 XQ1 QU3 WD10 XV2.0 QU5 XP3 IV6 XS2.1 XS3.1 XV3.0 SN XQ2 WD11 XQ3 TB MM0 MM1 WD12 QU6 IV7 MM2 IV8 MM3 WD13 MM4 QU7 QU8 MM5 IV9 SQ0.0 SQ0.1 MM6 RC0.0 RM0.0 SQ0.2 MM7 SQ0.3 RM0.1 AG0.0 WD14 RM0.2 AG0.1 RM0.3 AG0.2 FN0.0 RC0.1 WD15 RC0.2 MM8 RC0.3 AV0.3 QU9 IV10 MM9 FN0.1 FN0.2 IV11 FN0.3 SQ1.0 QU10 QU11 SQ1.1 MM10 RC1.0 RM1.0 SQ1.2 MM11 SQ1.3 RM1.1 AG1.0 WD16 RM1.2 AG1.1 RM1.3 AG1.2 WD17 RC1.1 RC1.2 RC1.3 AV1.3 IV12 FN1.0 FN1.1 IV13 FN1.2 WD18 QU12 QU13 MM12 IV14 MM13 FN1.3 IV15 WD19 QU14 QU15 MM14 SQ2.0 IV16 SQ2.1 MM15 RC2.0 SQ2.2 RM2.0 SQ2.3 RM2.1 AG2.0 SQ3.0 RM2.2 SQ3.1 AG2.1 FN2.0 RM2.3 SQ3.2 AG2.2 SQ3.3 RC2.1 RC2.2 RC2.3 AV2.3 FN2.1 QU16 FN2.2 IV17 MM16 FN2.3 IS20 IV18 QU17 QU18 MM17 IS21 RC3.0 RC3.1 RC3.2 RC3.3 IV19 MM18 RM3.0 RM3.1 AG3.0 RM3.2 AG3.1 FN3.0 RM3.3 AG3.2 FN3.1 QU19 FN3.2 AV3.3 MM19 QU20 FN3.3 QU21 MM20 IS23 IV22 MM21 QU22 SQ4.0 QU23 MM22 SQ4.1 RC4.0 RM4.0 MM23 SQ4.2 RM4.1 AG4.0 SQ4.3 OS1 RM4.2 AG4.1 FN4.0 OS3 RM4.3 AG4.2 RC4.1 RC4.2 RC4.3 FN4.1 AV4.3 FN4.2 OV0 FN4.3 OV2"
-DMA_ORDER = "q00 k0 q01 k1 q02 x0 q03 k2 q10 x1 q11 k3 q12 x2 q13 x3 g q20 q21 q22 q23 v0 q30 v1 q31 v2 q32 v3 q33"
+SEQ = "TR13 WD4 GM TR2 GE TR2 IV0 WD5 TR2 QU0 IV1 WD6 IV4 XP0 QU1 XS0.1 XV0.0 WD7 QU4 XQ0 IV2 XP1 WD8 IV5 XV1.0 XS1.1 QU2 WD9 IV3 XP2 XQ1 QU3 SN XS2.1 XV2.0 WD10 TB XP3 XQ2 XV3.0 XS3.1 QU5 WD11 XQ3 IV6 MM0 MM1 IV7 IS20 MM2 QU6 QU7 MM3 IV8 WD12 MM4 IV9 MM5 SQ0.0 QU8 SQ0.1 MM6 RC0.0 RM0.0 SQ0.2 MM7 RM0.1 SQ0.3 AG0.0 WD13 RM0.2 AG0.1 RM0.3 AG0.2 FN0.0 RC0.1 RC0.2 MM8 RC0.3 FN0.1 AV0.3 FN0.2 QU9 WD14 IV10 MM9 IV11 FN0.3 QU10 WD15 QU11 MM10 IV12 MM11 SQ1.0 IV13 SQ1.1 RC1.0 RM1.0 SQ1.2 SQ1.3 RM1.1 AG1.0 WD16 RM1.2 AG1.1 RM1.3 AG1.2 WD17 RC1.1 RC1.2 RC1.3 AV1.3 QU12 FN1.0 QU13 MM12 FN1.1 IV14 FN1.2 MM13 WD18 IV15 QU14 QU15 MM14 FN1.3 IV16 WD19 MM15 IV17 SQ2.0 QU16 SQ2.1 QU17 RC2.0 RM2.0 SQ2.2 SQ2.3 RM2.1 AG2.0 SQ3.0 RM2.2 SQ3.1 AG2.1 FN2.0 RM2.3 SQ3.2 AG2.2 SQ3.3 RC2.1 RC2.2 MM16 RC2.3 AV2.3 FN2.1 IV18 MM17 FN2.2 FN2.3 RC3.0 QU18 IS21 RC3.1 RC3.2 MM18 RC3.3 IV19 RM3.0 RM3.1 AG3.0 RM3.2 AG3.1 FN3.0 RM3.3 AG3.2 FN3.1 QU19 FN3.2 AV3.3 MM19 QU20 FN3.3 QU21 MM20 IS23 IV22 MM21 QU22 SQ4.0 QU23 MM22 SQ4.1 RC4.0 RM4.0 MM23 SQ4.2 RM4.1 AG4.0 SQ4.3 OS1 RM4.2 AG4.1 FN4.0 OS3 RM4.3 AG4.2 RC4.1 RC4.2 RC4.3 FN4.1 AV4.3 FN4.2 OV0 FN4.3 OV2"
+DMA_ORDER = "q00 g k0 q01 k1 q02 x0 q03 k2 q10 x1 q11 k3 q12 x2 q13 x3 q20 q21 q22 q23 v0 q30 v1 q31 v2 q32 v3 q33"
 CFG = {"WIDE_BUFS": 6, "GRP_BUFS": 3, "CODE_BUFS": 8}
 MANUAL = True
 
@@ -72,7 +72,12 @@ def tile_attention_pa_kernel(tc, x, wq_bytes, wq_scale, wk, wv, q_scale, k_scale
         for kind in ("k", "v"):
             for g in range(PASSES):
                 w_raw[(kind, g)] = raw.tile([P, PACK, NT], BF16, name="w%s_raw%d" % (kind, g))
-        gain = {"q": const.tile([P, HD], BF16, name="gain_q"), "k": const.tile([P, HD], BF16, name="gain_k")}
+        gain_rows = const.tile([P, 2 * HD], BF16, name="gain_rows")
+        nc.vector.memset(gain_rows[:], 0.0)
+        ones = const.tile([P, P], BF16, name="ones")
+        nc.vector.memset(ones[:], 1.0)
+        gain_all = const.tile([P, 2 * HD], F32, name="gain_all")
+        gain = {"q": gain_all[:, 0:HD], "k": gain_all[:, HD : 2 * HD]}
 
         def load_wq(j, g):
             nc.sync.dma_start(out=wq_b[(j, g)][:], in_=wqb_v[g][:, :, j * NT : (j + 1) * NT])
@@ -89,8 +94,8 @@ def tile_attention_pa_kernel(tc, x, wq_bytes, wq_scale, wk, wv, q_scale, k_scale
                 g = int(item[1])
                 nc.sync.dma_start(out=x_raw[g][:], in_=x_flat[g * P : (g + 1) * P, :])
             else:
-                nc.sync.dma_start(out=gain["q"][:], in_=q_scale.partition_broadcast(P))
-                nc.sync.dma_start(out=gain["k"][:], in_=k_scale.partition_broadcast(P))
+                nc.sync.dma_start(out=gain_rows[0:1, 0:HD], in_=q_scale.unsqueeze(0))
+                nc.sync.dma_start(out=gain_rows[0:1, HD : 2 * HD], in_=k_scale.unsqueeze(0))
 
         ident = const.tile([P, P], F32, name="ident")
         make_identity(nc, ident[:])
@@ -141,6 +146,14 @@ def tile_attention_pa_kernel(tc, x, wq_bytes, wq_scale, wk, wv, q_scale, k_scale
 
         tab_a = {}
         tab_b = {}
+        gain_bank = {}
+
+        def gain_spread():
+            gain_bank[0] = psum.tile([P, 2 * HD], F32, name="bank")
+            nc.tensor.matmul(out=gain_bank[0][:], lhsT=ones[:], rhs=gain_rows[:], start=True, stop=True)
+
+        def gain_evac():
+            nc.vector.tensor_copy(out=gain_all[:], in_=gain_bank[0][:])
 
         def build_tables():
             for kind in ("k", "q"):
@@ -305,6 +318,10 @@ def tile_attention_pa_kernel(tc, x, wq_bytes, wq_scale, wk, wv, q_scale, k_scale
                 sines()
             elif op == "TB":
                 build_tables()
+            elif op == "GM":
+                gain_spread()
+            elif op == "GE":
+                gain_evac()
             elif op == "WD":
                 widen(a[0])
             elif op == "IV":

@@ -16,13 +16,13 @@ ALU = mybir.AluOpType
 P = 128
 PACK = 4
 DM = 2048
-PASSES = 4
+PASSES = DM // (P * PACK)
 TOKENS = 512
-MT = 4
+TOKEN_TILES = TOKENS // P
 NT = 512
 HD = 128
-HALF = 64
-HEADS_PER_TILE = 4
+HALF = HD // 2
+HEADS = NT // HD
 THETA = 10000.0
 EPS = 1e-6
 PI = 3.141592653589793
@@ -31,21 +31,38 @@ TWO_PI_LO = 2.0 * PI - TWO_PI_HI
 
 FLOPS = 2 * TOKENS * DM * (2048 + 512 + 512)
 
-TILES = (("k", 0), ("q", 0), ("q", 1), ("q", 2), ("q", 3), ("v", 0))
-UNITS = len(TILES) * PASSES
-SEQ = "TR13 WD4 GM TR2 GE TR2 IV0 WD5 TR2 QU0 IV1 WD6 IV4 XP0 QU1 XS0.1 XV0.0 WD7 QU4 XQ0 IV2 XP1 WD8 IV5 XV1.0 XS1.1 QU2 WD9 IV3 XP2 XQ1 QU3 SN XS2.1 XV2.0 WD10 TB XP3 XQ2 XV3.0 XS3.1 QU5 WD11 XQ3 IV6 MM0 MM1 IV7 IS20 MM2 QU6 QU7 MM3 IV8 WD12 MM4 IV9 MM5 SQ0.0 QU8 SQ0.1 MM6 RC0.0 RM0.0 SQ0.2 MM7 RM0.1 SQ0.3 AG0.0 WD13 RM0.2 AG0.1 RM0.3 AG0.2 FN0.0 RC0.1 RC0.2 MM8 RC0.3 FN0.1 AV0.3 FN0.2 QU9 WD14 IV10 MM9 IV11 FN0.3 QU10 WD15 QU11 MM10 IV12 MM11 SQ1.0 IV13 SQ1.1 RC1.0 RM1.0 SQ1.2 SQ1.3 RM1.1 AG1.0 WD16 RM1.2 AG1.1 RM1.3 AG1.2 WD17 RC1.1 RC1.2 RC1.3 AV1.3 QU12 FN1.0 QU13 MM12 FN1.1 IV14 FN1.2 MM13 WD18 IV15 QU14 QU15 MM14 FN1.3 IV16 WD19 MM15 IV17 SQ2.0 QU16 SQ2.1 QU17 RC2.0 RM2.0 SQ2.2 SQ2.3 RM2.1 AG2.0 SQ3.0 RM2.2 SQ3.1 AG2.1 FN2.0 RM2.3 SQ3.2 AG2.2 SQ3.3 RC2.1 RC2.2 MM16 RC2.3 AV2.3 FN2.1 IV18 MM17 FN2.2 FN2.3 RC3.0 QU18 IS21 RC3.1 RC3.2 MM18 RC3.3 IV19 RM3.0 RM3.1 AG3.0 RM3.2 AG3.1 FN3.0 RM3.3 AG3.2 FN3.1 QU19 FN3.2 AV3.3 MM19 QU20 FN3.3 QU21 MM20 IS23 IV22 MM21 QU22 SQ4.0 QU23 MM22 SQ4.1 RC4.0 RM4.0 MM23 SQ4.2 RM4.1 AG4.0 SQ4.3 OS1 RM4.2 AG4.1 FN4.0 OS3 RM4.3 AG4.2 RC4.1 RC4.2 RC4.3 FN4.1 AV4.3 FN4.2 OV0 FN4.3 OV2"
-DMA_ORDER = "q00 g k0 q01 k1 q02 x0 q03 k2 q10 x1 q11 k3 q12 x2 q13 x3 q20 q21 q22 q23 v0 q30 v1 q31 v2 q32 v3 q33"
-CFG = {"WIDE_BUFS": 6, "GRP_BUFS": 3, "CODE_BUFS": 8}
-MANUAL = True
+COLUMN_TILES = (("k", 0), ("q", 0), ("q", 1), ("q", 2), ("q", 3), ("v", 0))
+UNITS = len(COLUMN_TILES) * PASSES
+NORMED_TILES = len(COLUMN_TILES) - 1
+FIRST_Q_UNIT = PASSES
+LAST_Q_UNIT = 5 * PASSES - 1
+
+WIDE_BUFS = 6
+SCALAR_UNITS = (20, 21, 23)
+SCALAR_COPY_LEAD = 6
+X_STEP = 3
+X_READY = X_STEP + TOKEN_TILES
+ROTATE_LAG = 10
+CHAIN_HEAD = 13
+CHAIN_PER_STEP = 2
+CHAIN_STEPS = 3
+TABLE_STEP = 5
+
+
+def rotated_in(step):
+    i, beyond = divmod(step - ROTATE_LAG, PASSES)
+    return i if (beyond == 0 and 0 <= i < NORMED_TILES - 1) else None
 
 
 def tile_attention_pa_kernel(tc, x, wq_bytes, wq_scale, wk, wv, q_scale, k_scale, out_0, out_1, out_2):
     nc = tc.nc
     x_flat = x.flatten_outer_dims()
-    wqb_v = wq_bytes.rearrange("(g p t) h d -> g p t (h d)", p=P, t=PACK)
-    wqs_v = wq_scale.rearrange("(g p t) a b -> p g (t a b)", p=P, t=PACK)
-    wk_v = wk.rearrange("(g p t) h d -> g p t (h d)", p=P, t=PACK)
-    wv_v = wv.rearrange("(g p t) h d -> g p t (h d)", p=P, t=PACK)
+    wq_bytes_v = wq_bytes.rearrange("(g p t) h d -> g p t (h d)", p=P, t=PACK)
+    wq_scale_v = wq_scale.rearrange("(g p t) a b -> p g (t a b)", p=P, t=PACK)
+    w_v = {
+        "k": wk.rearrange("(g p t) h d -> g p t (h d)", p=P, t=PACK),
+        "v": wv.rearrange("(g p t) h d -> g p t (h d)", p=P, t=PACK),
+    }
     dst = {
         "q": out_0.rearrange("b s h d -> (b s) (h d)"),
         "k": out_1.rearrange("b s h d -> (b s) (h d)"),
@@ -56,150 +73,139 @@ def tile_attention_pa_kernel(tc, x, wq_bytes, wq_scale, wk, wv, q_scale, k_scale
         const = ctx.enter_context(tc.tile_pool(name="const", bufs=1))
         raw = ctx.enter_context(tc.tile_pool(name="raw", bufs=1))
         keep = ctx.enter_context(tc.tile_pool(name="keep", bufs=1))
-        work = ctx.enter_context(tc.tile_pool(name="work", bufs=3))
+        work = ctx.enter_context(tc.tile_pool(name="work", bufs=2))
         psum = ctx.enter_context(tc.psum_pool(name="psum", bufs=8))
-        if MANUAL:
-            ctx.enter_context(tc.manual_schedule())
+        ctx.enter_context(tc.manual_schedule())
 
-        scl = const.tile([P, PASSES, PACK], F32, name="wq_scales")
-        nc.sync.dma_start(out=scl[:], in_=wqs_v)
-        x_raw = [raw.tile([P, DM], BF16, name="x_raw%d" % m) for m in range(MT)]
-        wq_b = {}
-        w_raw = {}
-        for j in range(4):
-            for g in range(PASSES):
-                wq_b[(j, g)] = raw.tile([P, PACK, NT], U8, name="wq_bytes_%d_%d" % (j, g))
-        for kind in ("k", "v"):
-            for g in range(PASSES):
-                w_raw[(kind, g)] = raw.tile([P, PACK, NT], BF16, name="w%s_raw%d" % (kind, g))
+        scales = const.tile([P, PASSES, PACK], F32, name="wq_scales")
         gain_rows = const.tile([P, 2 * HD], BF16, name="gain_rows")
         nc.vector.memset(gain_rows[:], 0.0)
-        ones = const.tile([P, P], BF16, name="ones")
-        nc.vector.memset(ones[:], 1.0)
-        gain_all = const.tile([P, 2 * HD], F32, name="gain_all")
-        gain = {"q": gain_all[:, 0:HD], "k": gain_all[:, HD : 2 * HD]}
+        x_raw = [raw.tile([P, DM], BF16, name="x_raw%d" % m) for m in range(TOKEN_TILES)]
+        wq_raw = {}
+        w_raw = {}
 
         def load_wq(j, g):
-            nc.sync.dma_start(out=wq_b[(j, g)][:], in_=wqb_v[g][:, :, j * NT : (j + 1) * NT])
+            wq_raw[(j, g)] = raw.tile([P, PACK, NT], U8, name="wq_bytes_%d_%d" % (j, g))
+            nc.sync.dma_start(out=wq_raw[(j, g)][:], in_=wq_bytes_v[g][:, :, j * NT : (j + 1) * NT])
 
-        for item in DMA_ORDER.split(" "):
-            kind0 = item[0]
-            if kind0 == "q":
-                load_wq(int(item[1]), int(item[2]))
-            elif kind0 == "k":
-                nc.sync.dma_start(out=w_raw[("k", int(item[1]))][:], in_=wk_v[int(item[1])])
-            elif kind0 == "v":
-                nc.sync.dma_start(out=w_raw[("v", int(item[1]))][:], in_=wv_v[int(item[1])])
-            elif kind0 == "x":
-                g = int(item[1])
-                nc.sync.dma_start(out=x_raw[g][:], in_=x_flat[g * P : (g + 1) * P, :])
-            else:
-                nc.sync.dma_start(out=gain_rows[0:1, 0:HD], in_=q_scale.unsqueeze(0))
-                nc.sync.dma_start(out=gain_rows[0:1, HD : 2 * HD], in_=k_scale.unsqueeze(0))
+        def load_w(kind, g):
+            w_raw[(kind, g)] = raw.tile([P, PACK, NT], BF16, name="w%s_raw%d" % (kind, g))
+            nc.sync.dma_start(out=w_raw[(kind, g)][:], in_=w_v[kind][g])
+
+        nc.sync.dma_start(out=scales[:], in_=wq_scale_v)
+        load_wq(0, 0)
+        nc.sync.dma_start(out=gain_rows[0:1, 0:HD], in_=q_scale.unsqueeze(0))
+        nc.sync.dma_start(out=gain_rows[0:1, HD : 2 * HD], in_=k_scale.unsqueeze(0))
+        for g in range(PASSES):
+            load_w("k", g)
+            if g + 1 < PASSES:
+                load_wq(0, g + 1)
+        for m in range(TOKEN_TILES):
+            nc.sync.dma_start(out=x_raw[m][:], in_=x_flat[m * P : (m + 1) * P, :])
+            load_wq(1, m)
+        for g in range(PASSES):
+            load_wq(2, g)
+        for g in range(PASSES):
+            load_w("v", g)
+            load_wq(3, g)
 
         ident = const.tile([P, P], F32, name="ident")
         make_identity(nc, ident[:])
+        ones = const.tile([P, P], BF16, name="ones")
+        nc.vector.memset(ones[:], 1.0)
+        zero = const.tile([P, 1], F32, name="zero")
+        nc.vector.memset(zero[:], 0.0)
+        unused = const.tile([P, 1], F32, name="unused")
+        nc.scalar.activation(out=unused[:], in_=zero[:], func=ACT.Sin)
 
-        zero1 = const.tile([P, 1], F32, name="zero1")
-        nc.vector.memset(zero1[:], 0.0)
-        warm = const.tile([P, 1], F32, name="warm")
-        nc.scalar.activation(out=warm[:], in_=zero1[:], func=ACT.Sin)
-        pos_i = const.tile([P, 2], I32, name="pos_i")
-        nc.gpsimd.iota(pos_i[:], pattern=[[P, 2]], base=0, channel_multiplier=1)
-        pos = const.tile([P, 2], F32, name="pos")
+        position_i = const.tile([P, 2], I32, name="position_i")
+        nc.gpsimd.iota(position_i[:], pattern=[[P, 2]], base=0, channel_multiplier=1)
+        position = const.tile([P, 2], F32, name="position")
         freq = const.tile([P, HALF], F32, name="freq")
-        arg = const.tile([P, 2, 2, HALF], F32, name="arg")
-        argf = arg[:].rearrange("p a j i -> p (a j i)")
-        turns_i = work.tile([P, 4 * HALF], I32, name="trig_tmp", bufs=7)
-        turns = work.tile([P, 4 * HALF], F32, name="trig_tmp", bufs=7)
-        red1 = work.tile([P, 4 * HALF], F32, name="trig_tmp", bufs=7)
-        red2 = work.tile([P, 4 * HALF], F32, name="trig_tmp", bufs=7)
-        over = work.tile([P, 4 * HALF], F32, name="trig_tmp", bufs=7)
-        red3 = work.tile([P, 4 * HALF], F32, name="trig_tmp", bufs=7)
-        red4 = work.tile([P, 4 * HALF], F32, name="trig_tmp", bufs=7)
-        trig = const.tile([P, 2, 2, HALF], F32, name="trig")
-        trig_ops = []
-        trig_ops.append(lambda: nc.vector.memset(freq[:, 0:1], 1.0))
-        trig_ops.append(lambda: nc.vector.tensor_copy(out=pos[:], in_=pos_i[:]))
+        angle = const.tile([P, 2, 2, HALF], F32, name="angle")
+        angle_flat = angle[:].rearrange("p a j i -> p (a j i)")
+        turns_i = const.tile([P, 4 * HALF], I32, name="turns_i")
+        turns = const.tile([P, 4 * HALF], F32, name="turns")
+        rest = [const.tile([P, 4 * HALF], F32, name="rest%d" % n) for n in range(4)]
+        above = const.tile([P, 4 * HALF], F32, name="above")
+        sines = const.tile([P, 2, 2, HALF], F32, name="sines")
+
+        def minus_turns(out, count, part, from_):
+            return lambda: nc.vector.scalar_tensor_tensor(out=out[:], in0=count[:], scalar=-part, in1=from_, op0=ALU.mult, op1=ALU.add)
+
+        chain = []
+        chain.append(lambda: nc.vector.memset(freq[:, 0:1], 1.0))
+        chain.append(lambda: nc.vector.tensor_copy(out=position[:], in_=position_i[:]))
         for b in range(6):
-            trig_ops.append(lambda w=(1 << b): nc.vector.tensor_scalar(out=freq[:, w : 2 * w], in0=freq[:, 0:w], scalar1=pow(THETA, -w / 64.0), scalar2=None, op0=ALU.mult))
+            chain.append(
+                lambda w=(1 << b): nc.vector.tensor_scalar(
+                    out=freq[:, w : 2 * w], in0=freq[:, 0:w], scalar1=pow(THETA, -w / 64.0), scalar2=None, op0=ALU.mult
+                )
+            )
         for j in range(2):
-            trig_ops.append(lambda j=j: nc.vector.tensor_scalar(out=arg[:, 0, j, :], in0=freq[:], scalar1=pos[:, j : j + 1], scalar2=None, op0=ALU.mult))
-            trig_ops.append(lambda j=j: nc.vector.tensor_scalar(out=arg[:, 1, j, :], in0=freq[:], scalar1=pos[:, j : j + 1], scalar2=PI / 2.0, op0=ALU.mult, op1=ALU.add))
-        trig_ops.append(lambda: nc.vector.tensor_scalar(out=turns_i[:], in0=argf, scalar1=1.0 / (2.0 * PI), scalar2=None, op0=ALU.mult))
-        trig_ops.append(lambda: nc.vector.tensor_copy(out=turns[:], in_=turns_i[:]))
-        trig_ops.append(lambda: nc.vector.scalar_tensor_tensor(out=red1[:], in0=turns[:], scalar=-TWO_PI_HI, in1=argf, op0=ALU.mult, op1=ALU.add))
-        trig_ops.append(lambda: nc.vector.scalar_tensor_tensor(out=red2[:], in0=turns[:], scalar=-TWO_PI_LO, in1=red1[:], op0=ALU.mult, op1=ALU.add))
-        trig_ops.append(lambda: nc.vector.tensor_scalar(out=over[:], in0=red2[:], scalar1=PI, scalar2=None, op0=ALU.is_gt))
-        trig_ops.append(lambda: nc.vector.scalar_tensor_tensor(out=red3[:], in0=over[:], scalar=-TWO_PI_HI, in1=red2[:], op0=ALU.mult, op1=ALU.add))
-        trig_ops.append(lambda: nc.vector.scalar_tensor_tensor(out=red4[:], in0=over[:], scalar=-TWO_PI_LO, in1=red3[:], op0=ALU.mult, op1=ALU.add))
+            chain.append(
+                lambda j=j: nc.vector.tensor_scalar(out=angle[:, 0, j, :], in0=freq[:], scalar1=position[:, j : j + 1], scalar2=None, op0=ALU.mult)
+            )
+            chain.append(
+                lambda j=j: nc.vector.tensor_scalar(
+                    out=angle[:, 1, j, :], in0=freq[:], scalar1=position[:, j : j + 1], scalar2=PI / 2.0, op0=ALU.mult, op1=ALU.add
+                )
+            )
+        chain.append(lambda: nc.vector.tensor_scalar(out=turns_i[:], in0=angle_flat, scalar1=1.0 / (2.0 * PI), scalar2=None, op0=ALU.mult))
+        chain.append(lambda: nc.vector.tensor_copy(out=turns[:], in_=turns_i[:]))
+        chain.append(minus_turns(rest[0], turns, TWO_PI_HI, angle_flat))
+        chain.append(minus_turns(rest[1], turns, TWO_PI_LO, rest[0][:]))
+        chain.append(lambda: nc.vector.tensor_scalar(out=above[:], in0=rest[1][:], scalar1=PI, scalar2=None, op0=ALU.is_gt))
+        chain.append(minus_turns(rest[2], above, TWO_PI_HI, rest[1][:]))
+        chain.append(minus_turns(rest[3], above, TWO_PI_LO, rest[2][:]))
+        assert len(chain) == CHAIN_HEAD + CHAIN_PER_STEP * CHAIN_STEPS
 
-        trig_done = [0]
+        def run_chain(first, last):
+            for link in chain[first:last]:
+                link()
 
-        def take_trig(n):
-            for i in range(trig_done[0], min(trig_done[0] + n, len(trig_ops))):
-                trig_ops[i]()
-            trig_done[0] = trig_done[0] + n
-
-        def sines():
-            nc.scalar.activation(out=trig[:].rearrange("p a j i -> p (a j i)"), in_=red4[:], func=ACT.Sin)
-
-        tab_a = {}
-        tab_b = {}
-        gain_bank = {}
-
-        def gain_spread():
-            gain_bank[0] = psum.tile([P, 2 * HD], F32, name="bank")
-            nc.tensor.matmul(out=gain_bank[0][:], lhsT=ones[:], rhs=gain_rows[:], start=True, stop=True)
-
-        def gain_evac():
-            nc.vector.tensor_copy(out=gain_all[:], in_=gain_bank[0][:])
+        gains = const.tile([P, 2 * HD], F32, name="gains")
+        gain = {"q": gains[:, 0:HD], "k": gains[:, HD : 2 * HD]}
+        table_same = {}
+        table_swap = {}
 
         def build_tables():
             for kind in ("k", "q"):
                 g = gain[kind]
                 for j in range(2):
-                    sin_j = trig[:, 0, j, :]
-                    cos_j = trig[:, 1, j, :]
-                    a = const.tile([P, HD], F32, name="tab_a_%s%d" % (kind, j))
-                    b = const.tile([P, HD], F32, name="tab_b_%s%d" % (kind, j))
-                    nc.vector.tensor_tensor(out=a[:, 0:HALF], in0=g[:, 0:HALF], in1=cos_j, op=ALU.mult)
-                    nc.vector.tensor_tensor(out=a[:, HALF:HD], in0=g[:, HALF:HD], in1=cos_j, op=ALU.mult)
-                    nc.vector.scalar_tensor_tensor(out=b[:, 0:HALF], in0=g[:, HALF:HD], scalar=-1.0, in1=sin_j, op0=ALU.mult, op1=ALU.mult)
-                    nc.vector.tensor_tensor(out=b[:, HALF:HD], in0=g[:, 0:HALF], in1=sin_j, op=ALU.mult)
-                    tab_a[(kind, j)] = a
-                    tab_b[(kind, j)] = b
+                    sin_j = sines[:, 0, j, :]
+                    cos_j = sines[:, 1, j, :]
+                    same = const.tile([P, HD], F32, name="table_same_%s%d" % (kind, j))
+                    swap = const.tile([P, HD], F32, name="table_swap_%s%d" % (kind, j))
+                    nc.vector.tensor_tensor(out=same[:, 0:HALF], in0=g[:, 0:HALF], in1=cos_j, op=ALU.mult)
+                    nc.vector.tensor_tensor(out=same[:, HALF:HD], in0=g[:, HALF:HD], in1=cos_j, op=ALU.mult)
+                    nc.vector.scalar_tensor_tensor(out=swap[:, 0:HALF], in0=g[:, HALF:HD], scalar=-1.0, in1=sin_j, op0=ALU.mult, op1=ALU.mult)
+                    nc.vector.tensor_tensor(out=swap[:, HALF:HD], in0=g[:, 0:HALF], in1=sin_j, op=ALU.mult)
+                    table_same[(kind, j)] = same
+                    table_swap[(kind, j)] = swap
 
-        x_codes = [keep.tile([P, PASSES * P], U32, name="x_codes%d" % m, align_bytes=64) for m in range(MT)]
-        x_scales = [keep.tile([P, PASSES * P], U8, name="x_scales%d" % m, align_bytes=64) for m in range(MT)]
-        x_grp = {}
+        x_codes = [keep.tile([P, PASSES * P], U32, name="x_codes%d" % m, align_bytes=64) for m in range(TOKEN_TILES)]
+        x_scales = [keep.tile([P, PASSES * P], U8, name="x_scales%d" % m, align_bytes=64) for m in range(TOKEN_TILES)]
+        x_grouped = {}
 
-        x_bank = {}
-
-        def x_trans(m):
+        def turn_x(m):
             words = x_raw[m][:].bitcast(F32)
-            for gp in range(2):
-                xt = psum.tile([P, 2, 2, P], F32, name="bank")
-                x_bank[(m, gp)] = xt
+            x_grouped[m] = work.tile([P, PASSES, P, PACK], BF16, name="x_grouped", bufs=2, align_bytes=64)
+            grouped_words = x_grouped[m][:].rearrange("p g r t -> p (g r t)").bitcast(F32).rearrange("p (g r u) -> p g r u", g=PASSES, u=2)
+            for half in range(2):
+                bank = psum.tile([P, 2, 2, P], F32, name="bank")
                 for g2 in range(2):
-                    g = 2 * gp + g2
+                    g = 2 * half + g2
                     for u in range(2):
-                        nc.tensor.transpose(xt[:, g2, u, :], words[:, 256 * g + u : 256 * (g + 1) : 2], ident[:])
+                        nc.tensor.transpose(bank[:, g2, u, :], words[:, 256 * g + u : 256 * (g + 1) : 2], ident[:])
+                src = bank[:].rearrange("p g u r -> p g r u")
+                if half == 0:
+                    nc.vector.tensor_copy(out=grouped_words[:, 0:2], in_=src)
+                else:
+                    nc.scalar.copy(out=grouped_words[:, 2:4], in_=src)
 
-        def x_evac(m, gp, on_scalar):
-            if m not in x_grp:
-                x_grp[m] = work.tile([P, PASSES, P, PACK], BF16, name="x_grp", bufs=2, align_bytes=64)
-            grp_words = x_grp[m][:].rearrange("p g r t -> p (g r t)").bitcast(F32).rearrange("p (g r u) -> p g r u", g=PASSES, u=2)
-            src = x_bank[(m, gp)][:].rearrange("p g u r -> p g r u")
-            if on_scalar:
-                nc.scalar.copy(out=grp_words[:, 2 * gp : 2 * gp + 2], in_=src)
-            else:
-                nc.vector.tensor_copy(out=grp_words[:, 2 * gp : 2 * gp + 2], in_=src)
-
-        def x_quant(m):
-            nc.vector.quantize_mx(
-                out=x_codes[m][:].bitcast(FP8X4), scales=x_scales[m][:], in_=x_grp[m][:].rearrange("p g r t -> p (g r t)")
-            )
+        def quantise_x(m):
+            nc.vector.quantize_mx(out=x_codes[m][:].bitcast(FP8X4), scales=x_scales[m][:], in_=x_grouped[m][:].rearrange("p g r t -> p (g r t)"))
 
         wide = {}
         grouped = {}
@@ -207,38 +213,39 @@ def tile_attention_pa_kernel(tc, x, wq_bytes, wq_scale, wk, wv, q_scale, k_scale
         w_scales = {}
 
         def widen(u):
-            kind, j = TILES[u // PASSES]
+            j = COLUMN_TILES[u // PASSES][1]
             g = u % PASSES
-            wd = work.tile([P, PACK, NT], BF16, name="wide", bufs=CFG["WIDE_BUFS"])
-            wide[u] = wd
+            wide[u] = work.tile([P, PACK, NT], BF16, name="wide", bufs=WIDE_BUFS)
             for t in range(PACK):
-                nc.scalar.activation(out=wd[:, t, :], in_=wq_b[(j, g)][:, t, :].bitcast(FP8), func=ACT.Copy, scale=scl[:, g, t : t + 1])
+                nc.scalar.activation(out=wide[u][:, t, :], in_=wq_raw[(j, g)][:, t, :].bitcast(FP8), func=ACT.Copy, scale=scales[:, g, t : t + 1])
 
-        def interleave(u, on_scalar):
-            kind, j = TILES[u // PASSES]
+        def interleave(u):
+            kind = COLUMN_TILES[u // PASSES][0]
             src = wide[u] if kind == "q" else w_raw[(kind, u % PASSES)]
-            grp = work.tile([P, NT, PACK], BF16, name=("grouped_s" if on_scalar else "grouped"), bufs=(2 if on_scalar else CFG["GRP_BUFS"]), align_bytes=64)
-            grouped[u] = grp
+            on_scalar = u in SCALAR_UNITS
+            grouped[u] = work.tile([P, NT, PACK], BF16, name=("grouped_by_scalar" if on_scalar else "grouped"), bufs=3, align_bytes=64)
+            out_view = grouped[u][:].rearrange("p (c i) t -> p c t i", i=4)
+            in_view = src[:].rearrange("p t (c i) -> p c t i", i=4)
             if on_scalar:
-                nc.scalar.copy(out=grp[:], in_=src[:].rearrange("p t n -> p n t"))
+                nc.scalar.copy(out=out_view, in_=in_view)
             else:
-                nc.vector.tensor_copy(out=grp[:], in_=src[:].rearrange("p t n -> p n t"))
+                nc.vector.tensor_copy(out=out_view, in_=in_view)
 
         def quantise(u):
-            w_codes[u] = work.tile([P, NT], U32, name="w_codes", bufs=CFG["CODE_BUFS"], align_bytes=64)
-            w_scales[u] = work.tile([P, NT], U8, name="w_scales", bufs=CFG["CODE_BUFS"], align_bytes=64)
+            w_codes[u] = work.tile([P, NT], U32, name="w_codes", bufs=8, align_bytes=64)
+            w_scales[u] = work.tile([P, NT], U8, name="w_scales", bufs=8, align_bytes=64)
             nc.vector.quantize_mx(out=w_codes[u][:].bitcast(FP8X4), scales=w_scales[u][:], in_=grouped[u][:].rearrange("p n t -> p (n t)"))
 
         acc = {}
 
         def multiply(u):
-            ti = u // PASSES
+            i = u // PASSES
             g = u % PASSES
-            for m in range(MT):
+            for m in range(TOKEN_TILES):
                 if g == 0:
-                    acc[(ti, m)] = psum.tile([P, NT], F32, name="bank")
+                    acc[(i, m)] = psum.tile([P, NT], F32, name="bank")
                 nc.tensor.matmul_mx(
-                    out=acc[(ti, m)][:],
+                    out=acc[(i, m)][:],
                     lhsT=x_codes[m][:, g * P : (g + 1) * P].bitcast(FP8X4),
                     lhsT_scale=x_scales[m][:, g * P : (g + 1) * P],
                     rhs=w_codes[u][:].bitcast(FP8X4),
@@ -247,114 +254,130 @@ def tile_attention_pa_kernel(tc, x, wq_bytes, wq_scale, wk, wv, q_scale, k_scale
                     stop=(g == PASSES - 1),
                 )
 
-        rstd = {}
-        rooted = {}
-        prod1 = {}
-        prod2 = {}
-        summed = {}
+        rms = {}
+        inv_rms = {}
+        product_same = {}
+        product_swap = {}
+        rotated = {}
 
-        def squares(ti, m):
-            ss = work.tile([P, HEADS_PER_TILE], F32, name="sumsq", bufs=12)
-            for h in range(HEADS_PER_TILE):
-                junk = work.tile([P, HD], BF16, name="junk", bufs=2)
-                nc.scalar.activation(out=junk[:], in_=acc[(ti, m)][:, h * HD : (h + 1) * HD], func=ACT.Square, accum_out=ss[:, h : h + 1])
-            rt = work.tile([P, HEADS_PER_TILE], F32, name="rooted", bufs=12)
-            nc.scalar.activation(out=rt[:], in_=ss[:], func=ACT.Sqrt, bias=EPS, scale=1.0 / HD)
-            rooted[(ti, m)] = rt
+        def sum_squares(i):
+            sums = work.tile([P, TOKEN_TILES * HEADS], F32, name="sums", bufs=2)
+            for m in range(TOKEN_TILES):
+                for h in range(HEADS):
+                    squares = work.tile([P, HD], BF16, name="squares", bufs=2)
+                    nc.scalar.activation(
+                        out=squares[:], in_=acc[(i, m)][:, h * HD : (h + 1) * HD], func=ACT.Square, accum_out=sums[:, m * HEADS + h : m * HEADS + h + 1]
+                    )
+            rms[i] = work.tile([P, TOKEN_TILES * HEADS], F32, name="rms", bufs=2)
+            nc.scalar.activation(out=rms[i][:], in_=sums[:], func=ACT.Sqrt, bias=EPS, scale=1.0 / HD)
 
-        def recip(ti, m):
-            r = work.tile([P, HEADS_PER_TILE], F32, name="rstd", bufs=12)
-            nc.vector.reciprocal(out=r[:], in_=rooted[(ti, m)][:])
-            rstd[(ti, m)] = r
-
-        def rope_mul(ti, m):
-            kind = TILES[ti][0]
-            a = tab_a[(kind, m % 2)]
-            b = tab_b[(kind, m % 2)]
-            u3 = acc[(ti, m)][:].rearrange("p (h d) -> p h d", h=HEADS_PER_TILE)
-            u4 = acc[(ti, m)][:].rearrange("p (h c i) -> p h c i", h=HEADS_PER_TILE, c=2)
-            t1 = work.tile([P, HEADS_PER_TILE, HD], F32, name="prod1", bufs=4)
-            t2 = work.tile([P, HEADS_PER_TILE, 2, HALF], F32, name="prod2", bufs=4)
-            nc.vector.tensor_tensor(out=t1[:], in0=u3, in1=a[:].unsqueeze(1).to_broadcast([P, HEADS_PER_TILE, HD]), op=ALU.mult)
-            nc.vector.tensor_tensor(
-                out=t2[:, :, 0, :], in0=u4[:, :, 1, :], in1=b[:, 0:HALF].unsqueeze(1).to_broadcast([P, HEADS_PER_TILE, HALF]), op=ALU.mult
-            )
-            nc.vector.tensor_tensor(
-                out=t2[:, :, 1, :], in0=u4[:, :, 0, :], in1=b[:, HALF:HD].unsqueeze(1).to_broadcast([P, HEADS_PER_TILE, HALF]), op=ALU.mult
-            )
-            prod1[(ti, m)] = t1
-            prod2[(ti, m)] = t2
-
-        def rope_add(ti, m, on_pool):
-            sm = work.tile([P, NT], F32, name=("summed_g" if on_pool else "summed_v"), bufs=(4 if on_pool else 2))
-            eng = nc.gpsimd if on_pool else nc.vector
-            eng.tensor_tensor(
-                out=sm[:], in0=prod1[(ti, m)][:].rearrange("p h d -> p (h d)"), in1=prod2[(ti, m)][:].rearrange("p h c i -> p (h c i)"), op=ALU.add
-            )
-            summed[(ti, m)] = sm
-
-        def finish(ti, m):
-            kind, j = TILES[ti]
-            y = work.tile([P, NT], F32, name="result", bufs=4)
-            for h in range(HEADS_PER_TILE):
-                nc.scalar.activation(
-                    out=y[:, h * HD : (h + 1) * HD], in_=summed[(ti, m)][:, h * HD : (h + 1) * HD], func=ACT.Copy, scale=rstd[(ti, m)][:, h : h + 1]
+        def multiply_tables(i, m):
+            kind = COLUMN_TILES[i][0]
+            same = table_same[(kind, m % 2)]
+            swap = table_swap[(kind, m % 2)]
+            by_head = acc[(i, m)][:].rearrange("p (h d) -> p h d", h=HEADS)
+            by_half = acc[(i, m)][:].rearrange("p (h c e) -> p h c e", h=HEADS, c=2)
+            product_same[(i, m)] = work.tile([P, HEADS, HD], F32, name="product_same", bufs=4)
+            product_swap[(i, m)] = work.tile([P, HEADS, 2, HALF], F32, name="product_swap", bufs=4)
+            nc.vector.tensor_tensor(out=product_same[(i, m)][:], in0=by_head, in1=same[:].unsqueeze(1).to_broadcast([P, HEADS, HD]), op=ALU.mult)
+            for c in range(2):
+                nc.vector.tensor_tensor(
+                    out=product_swap[(i, m)][:, :, c, :],
+                    in0=by_half[:, :, 1 - c, :],
+                    in1=swap[:, c * HALF : (c + 1) * HALF].unsqueeze(1).to_broadcast([P, HEADS, HALF]),
+                    op=ALU.mult,
                 )
-            nc.sync.dma_start(out=dst[kind][m * P : (m + 1) * P, j * NT : (j + 1) * NT], in_=y[:])
 
-        def v_out(ti, m, on_vector):
-            y = work.tile([P, NT], F32, name=("summed_v" if on_vector else "result"), bufs=(2 if on_vector else 4))
-            if on_vector:
-                nc.vector.tensor_copy(out=y[:], in_=acc[(ti, m)][:])
-            else:
-                nc.scalar.copy(out=y[:], in_=acc[(ti, m)][:])
-            nc.sync.dma_start(out=dst["v"][m * P : (m + 1) * P, :], in_=y[:])
+        def add_products(i, m, engine, ring, bufs):
+            rotated[(i, m)] = work.tile([P, NT], F32, name=ring, bufs=bufs)
+            engine.tensor_tensor(
+                out=rotated[(i, m)][:],
+                in0=product_same[(i, m)][:].rearrange("p h d -> p (h d)"),
+                in1=product_swap[(i, m)][:].rearrange("p h c e -> p (h c e)"),
+                op=ALU.add,
+            )
 
-        for tok in SEQ.split(" "):
-            op, a = tok[0:2], [int(z) for z in tok[2:].split(".") if z != ""]
-            if op == "TR":
-                take_trig(a[0])
-            elif op == "SN":
-                sines()
-            elif op == "TB":
+        def rotate(i):
+            inv_rms[i] = work.tile([P, TOKEN_TILES * HEADS], F32, name="inv_rms", bufs=2)
+            nc.vector.reciprocal(out=inv_rms[i][:], in_=rms[i][:])
+            for m in range(TOKEN_TILES):
+                multiply_tables(i, m)
+                if m >= 1:
+                    add_products(i, m - 1, nc.gpsimd, "rotated_by_gpsimd", 4)
+
+        def add_last(i):
+            add_products(i, TOKEN_TILES - 1, nc.vector, "rotated_by_vector", 2)
+
+        def finish(i, m):
+            kind, j = COLUMN_TILES[i]
+            result = work.tile([P, NT], F32, name="result", bufs=4)
+            for h in range(HEADS):
+                nc.scalar.activation(
+                    out=result[:, h * HD : (h + 1) * HD],
+                    in_=rotated[(i, m)][:, h * HD : (h + 1) * HD],
+                    func=ACT.Copy,
+                    scale=inv_rms[i][:, m * HEADS + h : m * HEADS + h + 1],
+                )
+            nc.sync.dma_start(out=dst[kind][m * P : (m + 1) * P, j * NT : (j + 1) * NT], in_=result[:])
+
+        def store_v(m):
+            v_result = work.tile([P, NT], F32, name="v_result", bufs=4)
+            nc.scalar.copy(out=v_result[:], in_=acc[(len(COLUMN_TILES) - 1, m)][:])
+            nc.sync.dma_start(out=dst["v"][m * P : (m + 1) * P, :], in_=v_result[:])
+
+        gain_bank = psum.tile([P, 2 * HD], F32, name="bank")
+        nc.tensor.matmul(out=gain_bank[:], lhsT=ones[:], rhs=gain_rows[:], start=True, stop=True)
+        run_chain(0, CHAIN_HEAD)
+        for u in range(FIRST_Q_UNIT, FIRST_Q_UNIT + PASSES):
+            widen(u)
+        add_waiting = []
+        for s in range(UNITS + 1):
+            if s < UNITS and s not in SCALAR_UNITS:
+                interleave(s)
+            for i in add_waiting:
+                add_last(i)
+            add_waiting = []
+            if s == 0:
+                nc.vector.tensor_copy(out=gains[:], in_=gain_bank[:])
+            if s >= 1:
+                quantise(s - 1)
+            if s < CHAIN_STEPS:
+                run_chain(CHAIN_HEAD + CHAIN_PER_STEP * s, CHAIN_HEAD + CHAIN_PER_STEP * (s + 1))
+            if X_STEP < s <= X_READY:
+                quantise_x(s - X_STEP - 1)
+            if X_STEP <= s < X_READY:
+                turn_x(s - X_STEP)
+            if s == TABLE_STEP:
                 build_tables()
-            elif op == "GM":
-                gain_spread()
-            elif op == "GE":
-                gain_evac()
-            elif op == "WD":
-                widen(a[0])
-            elif op == "IV":
-                interleave(a[0], False)
-            elif op == "IS":
-                interleave(a[0], True)
-            elif op == "QU":
-                quantise(a[0])
-            elif op == "MM":
-                multiply(a[0])
-            elif op == "XP":
-                x_trans(a[0])
-            elif op == "XV":
-                x_evac(a[0], a[1], False)
-            elif op == "XS":
-                x_evac(a[0], a[1], True)
-            elif op == "XQ":
-                x_quant(a[0])
-            elif op == "SQ":
-                squares(a[0], a[1])
-            elif op == "RC":
-                recip(a[0], a[1])
-            elif op == "RM":
-                rope_mul(a[0], a[1])
-            elif op == "AV":
-                rope_add(a[0], a[1], False)
-            elif op == "AG":
-                rope_add(a[0], a[1], True)
-            elif op == "FN":
-                finish(a[0], a[1])
-            elif op == "OV":
-                v_out(len(TILES) - 1, a[0], True)
-            elif op == "OS":
-                v_out(len(TILES) - 1, a[0], False)
-            else:
-                raise ValueError(tok)
+            i = rotated_in(s)
+            if i is not None:
+                rotate(i)
+                add_waiting.append(i)
+            if s == X_READY:
+                for u in range(s - 1):
+                    multiply(u)
+            elif s > X_READY:
+                multiply(s - 2)
+            if s == CHAIN_STEPS - 1:
+                nc.scalar.activation(out=sines[:].rearrange("p a j i -> p (a j i)"), in_=rest[3][:], func=ACT.Sin)
+                nc.scalar.activation(out=unused[:], in_=freq[:, 0:1], func=ACT.Sqrt)
+            if s == X_READY + 1:
+                sum_squares(0)
+            if i is not None:
+                sum_squares(i + 1)
+                for m in range(TOKEN_TILES - 1):
+                    finish(i, m)
+            if rotated_in(s - 1) is not None:
+                finish(rotated_in(s - 1), TOKEN_TILES - 1)
+            if 2 <= s and s + WIDE_BUFS <= LAST_Q_UNIT:
+                widen(s + WIDE_BUFS)
+            if s + SCALAR_COPY_LEAD in SCALAR_UNITS:
+                interleave(s + SCALAR_COPY_LEAD)
+        multiply(UNITS - 1)
+        for m in range(TOKEN_TILES):
+            store_v(m)
+        rotate(NORMED_TILES - 1)
+        for m in range(TOKEN_TILES - 1):
+            finish(NORMED_TILES - 1, m)
+        add_last(NORMED_TILES - 1)
+        finish(NORMED_TILES - 1, TOKEN_TILES - 1)

@@ -74,7 +74,7 @@ def tile_attention_pa_kernel(tc, x, wq_bytes, wq_scale, wk, wv, q_scale, k_scale
         raw = ctx.enter_context(tc.tile_pool(name="raw", bufs=1))
         keep = ctx.enter_context(tc.tile_pool(name="keep", bufs=1))
         work = ctx.enter_context(tc.tile_pool(name="work", bufs=2))
-        psum = ctx.enter_context(tc.psum_pool(name="psum", bufs=8))
+        psum = ctx.enter_context(tc.psum_pool(name="psum", bufs=1))
         ctx.enter_context(tc.manual_schedule())
 
         scales = const.tile([P, PASSES, PACK], F32, name="wq_scales")
@@ -84,16 +84,17 @@ def tile_attention_pa_kernel(tc, x, wq_bytes, wq_scale, wk, wv, q_scale, k_scale
         wq_raw = {}
         w_raw = {}
 
-        def load_wq(j, g):
+        def load_wq(j, g, cuts=(0, PACK)):
             wq_raw[(j, g)] = raw.tile([P, PACK, NT], U8, name="wq_bytes_%d_%d" % (j, g))
-            nc.sync.dma_start(out=wq_raw[(j, g)][:], in_=wq_bytes_v[g][:, :, j * NT : (j + 1) * NT])
+            for t0, t1 in zip(cuts[:-1], cuts[1:]):
+                nc.sync.dma_start(out=wq_raw[(j, g)][:, t0:t1, :], in_=wq_bytes_v[g][:, t0:t1, j * NT : (j + 1) * NT])
 
         def load_w(kind, g):
             w_raw[(kind, g)] = raw.tile([P, PACK, NT], BF16, name="w%s_raw%d" % (kind, g))
             nc.sync.dma_start(out=w_raw[(kind, g)][:], in_=w_v[kind][g])
 
         nc.sync.dma_start(out=scales[:], in_=wq_scale_v)
-        load_wq(0, 0)
+        load_wq(0, 0, cuts=(0, 1, PACK))
         nc.sync.dma_start(out=gain_rows[0:1, 0:HD], in_=q_scale.unsqueeze(0))
         nc.sync.dma_start(out=gain_rows[0:1, HD : 2 * HD], in_=k_scale.unsqueeze(0))
         for g in range(PASSES):
@@ -193,7 +194,7 @@ def tile_attention_pa_kernel(tc, x, wq_bytes, wq_scale, wk, wv, q_scale, k_scale
             x_grouped[m] = work.tile([P, PASSES, P, PACK], BF16, name="x_grouped", bufs=2, align_bytes=64)
             grouped_words = x_grouped[m][:].rearrange("p g r t -> p (g r t)").bitcast(F32).rearrange("p (g r u) -> p g r u", g=PASSES, u=2)
             for half in range(2):
-                bank = psum.tile([P, 2, 2, P], F32, name="bank")
+                bank = psum.tile([P, 2, 2, P], F32, name="bank%d" % (4 + 2 * (m % 2) + half))
                 for g2 in range(2):
                     g = 2 * half + g2
                     for u in range(2):
@@ -238,21 +239,20 @@ def tile_attention_pa_kernel(tc, x, wq_bytes, wq_scale, wk, wv, q_scale, k_scale
 
         acc = {}
 
-        def multiply(u):
+        def multiply(u, m):
             i = u // PASSES
             g = u % PASSES
-            for m in range(TOKEN_TILES):
-                if g == 0:
-                    acc[(i, m)] = psum.tile([P, NT], F32, name="bank")
-                nc.tensor.matmul_mx(
-                    out=acc[(i, m)][:],
-                    lhsT=x_codes[m][:, g * P : (g + 1) * P].bitcast(FP8X4),
-                    lhsT_scale=x_scales[m][:, g * P : (g + 1) * P],
-                    rhs=w_codes[u][:].bitcast(FP8X4),
-                    rhs_scale=w_scales[u][:],
-                    start=(g == 0),
-                    stop=(g == PASSES - 1),
-                )
+            if g == 0:
+                acc[(i, m)] = psum.tile([P, NT], F32, name="bank%d" % (TOKEN_TILES * (i % 2) + m))
+            nc.tensor.matmul_mx(
+                out=acc[(i, m)][:],
+                lhsT=x_codes[m][:, g * P : (g + 1) * P].bitcast(FP8X4),
+                lhsT_scale=x_scales[m][:, g * P : (g + 1) * P],
+                rhs=w_codes[u][:].bitcast(FP8X4),
+                rhs_scale=w_scales[u][:],
+                start=(g == 0),
+                stop=(g == PASSES - 1),
+            )
 
         rms = {}
         inv_rms = {}
@@ -325,7 +325,7 @@ def tile_attention_pa_kernel(tc, x, wq_bytes, wq_scale, wk, wv, q_scale, k_scale
             nc.scalar.copy(out=v_result[:], in_=acc[(len(COLUMN_TILES) - 1, m)][:])
             nc.sync.dma_start(out=dst["v"][m * P : (m + 1) * P, :], in_=v_result[:])
 
-        gain_bank = psum.tile([P, 2 * HD], F32, name="bank")
+        gain_bank = psum.tile([P, 2 * HD], F32, name="bank3")
         nc.tensor.matmul(out=gain_bank[:], lhsT=ones[:], rhs=gain_rows[:], start=True, stop=True)
         run_chain(0, CHAIN_HEAD)
         for u in range(FIRST_Q_UNIT, FIRST_Q_UNIT + PASSES):
@@ -353,11 +353,10 @@ def tile_attention_pa_kernel(tc, x, wq_bytes, wq_scale, wk, wv, q_scale, k_scale
             if i is not None:
                 rotate(i)
                 add_waiting.append(i)
-            if s == X_READY:
-                for u in range(s - 1):
-                    multiply(u)
-            elif s > X_READY:
-                multiply(s - 2)
+            for u in range(s - 1):
+                for m in range(TOKEN_TILES):
+                    if max(u + 2, X_STEP + 1 + m) == s:
+                        multiply(u, m)
             if s == CHAIN_STEPS - 1:
                 nc.scalar.activation(out=sines[:].rearrange("p a j i -> p (a j i)"), in_=rest[3][:], func=ACT.Sin)
                 nc.scalar.activation(out=unused[:], in_=freq[:, 0:1], func=ACT.Sqrt)
@@ -373,7 +372,8 @@ def tile_attention_pa_kernel(tc, x, wq_bytes, wq_scale, wk, wv, q_scale, k_scale
                 widen(s + WIDE_BUFS)
             if s + SCALAR_COPY_LEAD in SCALAR_UNITS:
                 interleave(s + SCALAR_COPY_LEAD)
-        multiply(UNITS - 1)
+        for m in range(TOKEN_TILES):
+            multiply(UNITS - 1, m)
         for m in range(TOKEN_TILES):
             store_v(m)
         rotate(NORMED_TILES - 1)

@@ -166,24 +166,22 @@ def tile_attention_pa_kernel(tc, x, wq_bytes, wq_scale, wk, wv, q_scale, k_scale
                 link()
 
         gains = const.tile([P, 2 * HD], F32, name="gains")
-        gain = {"q": gains[:, 0:HD], "k": gains[:, HD : 2 * HD]}
-        table_same = {}
-        table_swap = {}
+        gains_by_half = gains[:].rearrange("p (k c e) -> p k c e", k=2, c=2)
+        KIND_INDEX = {"q": 0, "k": 1}
+        tables = const.tile([P, 2, 2, 2, 2, HALF], F32, name="tables")
 
         def build_tables():
-            for kind in ("k", "q"):
-                g = gain[kind]
-                for j in range(2):
-                    sin_j = sines[:, 0, j, :]
-                    cos_j = sines[:, 1, j, :]
-                    same = const.tile([P, HD], F32, name="table_same_%s%d" % (kind, j))
-                    swap = const.tile([P, HD], F32, name="table_swap_%s%d" % (kind, j))
-                    nc.vector.tensor_tensor(out=same[:, 0:HALF], in0=g[:, 0:HALF], in1=cos_j, op=ALU.mult)
-                    nc.vector.tensor_tensor(out=same[:, HALF:HD], in0=g[:, HALF:HD], in1=cos_j, op=ALU.mult)
-                    nc.vector.scalar_tensor_tensor(out=swap[:, 0:HALF], in0=g[:, HALF:HD], scalar=-1.0, in1=sin_j, op0=ALU.mult, op1=ALU.mult)
-                    nc.vector.tensor_tensor(out=swap[:, HALF:HD], in0=g[:, 0:HALF], in1=sin_j, op=ALU.mult)
-                    table_same[(kind, j)] = same
-                    table_swap[(kind, j)] = swap
+            for j in range(2):
+                sin_j = sines[:, 0, j, :]
+                cos_j = sines[:, 1, j, :]
+                nc.vector.tensor_tensor(
+                    out=tables[:, :, j, 0, :, :], in0=gains_by_half, in1=cos_j.unsqueeze(1).unsqueeze(1).to_broadcast([P, 2, 2, HALF]), op=ALU.mult
+                )
+                sin_both = sin_j.unsqueeze(1).to_broadcast([P, 2, HALF])
+                nc.vector.tensor_tensor(out=tables[:, :, j, 1, 0, :], in0=gains_by_half[:, :, 0, :], in1=sin_both, op=ALU.mult)
+                nc.vector.scalar_tensor_tensor(
+                    out=tables[:, :, j, 1, 1, :], in0=gains_by_half[:, :, 1, :], scalar=-1.0, in1=sin_both, op0=ALU.mult, op1=ALU.mult
+                )
 
         x_codes = [keep.tile([P, PASSES * P], U32, name="x_codes%d" % m, align_bytes=64) for m in range(TOKEN_TILES)]
         x_scales = [keep.tile([P, PASSES * P], U8, name="x_scales%d" % m, align_bytes=64) for m in range(TOKEN_TILES)]
@@ -256,9 +254,7 @@ def tile_attention_pa_kernel(tc, x, wq_bytes, wq_scale, wk, wv, q_scale, k_scale
 
         rms = {}
         inv_rms = {}
-        product_same = {}
-        product_swap = {}
-        rotated = {}
+        products = {}
 
         def sum_squares(i):
             sums = work.tile([P, TOKEN_TILES * HEADS], F32, name="sums", bufs=2)
@@ -273,29 +269,23 @@ def tile_attention_pa_kernel(tc, x, wq_bytes, wq_scale, wk, wv, q_scale, k_scale
 
         def multiply_tables(i, m):
             kind = COLUMN_TILES[i][0]
-            same = table_same[(kind, m % 2)]
-            swap = table_swap[(kind, m % 2)]
-            by_head = acc[(i, m)][:].rearrange("p (h d) -> p h d", h=HEADS)
-            by_half = acc[(i, m)][:].rearrange("p (h c e) -> p h c e", h=HEADS, c=2)
-            product_same[(i, m)] = work.tile([P, HEADS, HD], F32, name="product_same", bufs=4)
-            product_swap[(i, m)] = work.tile([P, HEADS, 2, HALF], F32, name="product_swap", bufs=4)
-            nc.vector.tensor_tensor(out=product_same[(i, m)][:], in0=by_head, in1=same[:].unsqueeze(1).to_broadcast([P, HEADS, HD]), op=ALU.mult)
-            for c in range(2):
-                nc.vector.tensor_tensor(
-                    out=product_swap[(i, m)][:, :, c, :],
-                    in0=by_half[:, :, 1 - c, :],
-                    in1=swap[:, c * HALF : (c + 1) * HALF].unsqueeze(1).to_broadcast([P, HEADS, HALF]),
-                    op=ALU.mult,
+            table = tables[:, KIND_INDEX[kind], m % 2, :, :, :].rearrange("p w c e -> p w (c e)")
+            products[(i, m)] = work.tile([P, HEADS, 2, 2, HALF], F32, name="products", bufs=4)
+            for h in range(HEADS):
+                nc.vector.scalar_tensor_tensor(
+                    out=products[(i, m)][:, h, :, :, :].rearrange("p w c e -> p w (c e)"),
+                    in0=acc[(i, m)][:, h * HD : (h + 1) * HD].unsqueeze(1).to_broadcast([P, 2, HD]),
+                    scalar=inv_rms[i][:, m * HEADS + h : m * HEADS + h + 1],
+                    in1=table,
+                    op0=ALU.mult,
+                    op1=ALU.mult,
                 )
 
         def add_products(i, m, engine, ring, bufs):
-            rotated[(i, m)] = work.tile([P, NT], F32, name=ring, bufs=bufs)
-            engine.tensor_tensor(
-                out=rotated[(i, m)][:],
-                in0=product_same[(i, m)][:].rearrange("p h d -> p (h d)"),
-                in1=product_swap[(i, m)][:].rearrange("p h c e -> p (h c e)"),
-                op=ALU.add,
-            )
+            kind, j = COLUMN_TILES[i]
+            result = work.tile([P, HEADS, 2, HALF], F32, name=ring, bufs=bufs)
+            engine.tensor_tensor(out=result[:], in0=products[(i, m)][:, :, 0, :, :], in1=products[(i, m)][:, :, 1, ::-1, :], op=ALU.add)
+            nc.sync.dma_start(out=dst[kind][m * P : (m + 1) * P, j * NT : (j + 1) * NT], in_=result[:].rearrange("p h c e -> p (h c e)"))
 
         def rotate(i):
             inv_rms[i] = work.tile([P, TOKEN_TILES * HEADS], F32, name="inv_rms", bufs=2)
@@ -303,22 +293,10 @@ def tile_attention_pa_kernel(tc, x, wq_bytes, wq_scale, wk, wv, q_scale, k_scale
             for m in range(TOKEN_TILES):
                 multiply_tables(i, m)
                 if m >= 1:
-                    add_products(i, m - 1, nc.gpsimd, "rotated_by_gpsimd", 4)
+                    add_products(i, m - 1, nc.gpsimd, "result_by_gpsimd", 4)
 
         def add_last(i):
-            add_products(i, TOKEN_TILES - 1, nc.vector, "rotated_by_vector", 2)
-
-        def finish(i, m):
-            kind, j = COLUMN_TILES[i]
-            result = work.tile([P, NT], F32, name="result", bufs=4)
-            for h in range(HEADS):
-                nc.scalar.activation(
-                    out=result[:, h * HD : (h + 1) * HD],
-                    in_=rotated[(i, m)][:, h * HD : (h + 1) * HD],
-                    func=ACT.Copy,
-                    scale=inv_rms[i][:, m * HEADS + h : m * HEADS + h + 1],
-                )
-            nc.sync.dma_start(out=dst[kind][m * P : (m + 1) * P, j * NT : (j + 1) * NT], in_=result[:])
+            add_products(i, TOKEN_TILES - 1, nc.vector, "result_by_vector", 2)
 
         def store_v(m):
             v_result = work.tile([P, NT], F32, name="v_result", bufs=4)
@@ -364,10 +342,6 @@ def tile_attention_pa_kernel(tc, x, wq_bytes, wq_scale, wk, wv, q_scale, k_scale
                 sum_squares(0)
             if i is not None:
                 sum_squares(i + 1)
-                for m in range(TOKEN_TILES - 1):
-                    finish(i, m)
-            if rotated_in(s - 1) is not None:
-                finish(rotated_in(s - 1), TOKEN_TILES - 1)
             if 2 <= s and s + WIDE_BUFS <= LAST_Q_UNIT:
                 widen(s + WIDE_BUFS)
             if s + SCALAR_COPY_LEAD in SCALAR_UNITS:
@@ -377,7 +351,4 @@ def tile_attention_pa_kernel(tc, x, wq_bytes, wq_scale, wk, wv, q_scale, k_scale
         for m in range(TOKEN_TILES):
             store_v(m)
         rotate(NORMED_TILES - 1)
-        for m in range(TOKEN_TILES - 1):
-            finish(NORMED_TILES - 1, m)
         add_last(NORMED_TILES - 1)
-        finish(NORMED_TILES - 1, TOKEN_TILES - 1)

@@ -38,8 +38,8 @@ FIRST_Q_UNIT = PASSES
 LAST_Q_UNIT = 5 * PASSES - 1
 
 WIDE_BUFS = 6
-SCALAR_UNITS = (20, 21, 23)
-SCALAR_COPY_LEAD = 6
+SCALAR_UNITS = (18, 19, 20, 21, 22, 23)
+SCALAR_COPY_LEAD = 4
 X_STEP = 3
 X_READY = X_STEP + TOKEN_TILES
 ROTATE_LAG = 10

@@ -222,7 +222,10 @@ def tile_attention_pa_kernel(tc, x, wq_bytes, wq_scale, wk, wv, q_scale, k_scale
             kind = COLUMN_TILES[u // PASSES][0]
             src = wide[u] if kind == "q" else w_raw[(kind, u % PASSES)]
             on_scalar = u in SCALAR_UNITS
-            grouped[u] = work.tile([P, NT, PACK], BF16, name=("grouped_by_scalar" if on_scalar else "grouped"), bufs=3, align_bytes=64)
+            if on_scalar:
+                grouped[u] = work.tile([P, NT, PACK], BF16, name="grouped_by_scalar", bufs=len(SCALAR_UNITS), align_bytes=64)
+            else:
+                grouped[u] = work.tile([P, NT, PACK], BF16, name="grouped", bufs=3, align_bytes=64)
             out_view = grouped[u][:].rearrange("p (c i) t -> p c t i", i=4)
             in_view = src[:].rearrange("p t (c i) -> p c t i", i=4)
             if on_scalar:

@@ -43,9 +43,9 @@ SCALAR_COPY_LEAD = 4
 X_STEP = 3
 X_READY = X_STEP + TOKEN_TILES
 ROTATE_LAG = 10
-CHAIN_HEAD = 13
+CHAIN_HEAD = 12
 CHAIN_PER_STEP = 2
-CHAIN_STEPS = 3
+CHAIN_STEPS = 2
 TABLE_STEP = 5
 
 
@@ -127,8 +127,7 @@ def tile_attention_pa_kernel(tc, x, wq_bytes, wq_scale, wk, wv, q_scale, k_scale
         angle_flat = angle[:].rearrange("p a j i -> p (a j i)")
         turns_i = const.tile([P, 4 * HALF], I32, name="turns_i")
         turns = const.tile([P, 4 * HALF], F32, name="turns")
-        rest = [const.tile([P, 4 * HALF], F32, name="rest%d" % n) for n in range(4)]
-        above = const.tile([P, 4 * HALF], F32, name="above")
+        rest = [const.tile([P, 4 * HALF], F32, name="rest%d" % n) for n in range(2)]
         sines = const.tile([P, 2, 2, HALF], F32, name="sines")
 
         def minus_turns(out, count, part, from_):
@@ -156,9 +155,6 @@ def tile_attention_pa_kernel(tc, x, wq_bytes, wq_scale, wk, wv, q_scale, k_scale
         chain.append(lambda: nc.vector.tensor_copy(out=turns[:], in_=turns_i[:]))
         chain.append(minus_turns(rest[0], turns, TWO_PI_HI, angle_flat))
         chain.append(minus_turns(rest[1], turns, TWO_PI_LO, rest[0][:]))
-        chain.append(lambda: nc.vector.tensor_scalar(out=above[:], in0=rest[1][:], scalar1=PI, scalar2=None, op0=ALU.is_gt))
-        chain.append(minus_turns(rest[2], above, TWO_PI_HI, rest[1][:]))
-        chain.append(minus_turns(rest[3], above, TWO_PI_LO, rest[2][:]))
         assert len(chain) == CHAIN_HEAD + CHAIN_PER_STEP * CHAIN_STEPS
 
         def run_chain(first, last):
@@ -198,10 +194,7 @@ def tile_attention_pa_kernel(tc, x, wq_bytes, wq_scale, wk, wv, q_scale, k_scale
                     for u in range(2):
                         nc.tensor.transpose(bank[:, g2, u, :], words[:, 256 * g + u : 256 * (g + 1) : 2], ident[:])
                 src = bank[:].rearrange("p g u r -> p g r u")
-                if half == 0:
-                    nc.vector.tensor_copy(out=grouped_words[:, 0:2], in_=src)
-                else:
-                    nc.scalar.copy(out=grouped_words[:, 2:4], in_=src)
+                nc.vector.tensor_copy(out=grouped_words[:, 2 * half : 2 * half + 2], in_=src)
 
         def quantise_x(m):
             nc.vector.quantize_mx(out=x_codes[m][:].bitcast(FP8X4), scales=x_scales[m][:], in_=x_grouped[m][:].rearrange("p g r t -> p (g r t)"))
@@ -255,7 +248,6 @@ def tile_attention_pa_kernel(tc, x, wq_bytes, wq_scale, wk, wv, q_scale, k_scale
                 stop=(g == PASSES - 1),
             )
 
-        rms = {}
         inv_rms = {}
         products = {}
 
@@ -267,8 +259,8 @@ def tile_attention_pa_kernel(tc, x, wq_bytes, wq_scale, wk, wv, q_scale, k_scale
                     nc.scalar.activation(
                         out=squares[:], in_=acc[(i, m)][:, h * HD : (h + 1) * HD], func=ACT.Square, accum_out=sums[:, m * HEADS + h : m * HEADS + h + 1]
                     )
-            rms[i] = work.tile([P, TOKEN_TILES * HEADS], F32, name="rms", bufs=2)
-            nc.scalar.activation(out=rms[i][:], in_=sums[:], func=ACT.Sqrt, bias=EPS, scale=1.0 / HD)
+            inv_rms[i] = work.tile([P, TOKEN_TILES * HEADS], F32, name="inv_rms", bufs=2)
+            nc.scalar.activation(out=inv_rms[i][:], in_=sums[:], func=ACT.Abs_reciprocal_sqrt, bias=EPS, scale=1.0 / HD)
 
         def multiply_tables(i, m):
             kind = COLUMN_TILES[i][0]
@@ -291,8 +283,6 @@ def tile_attention_pa_kernel(tc, x, wq_bytes, wq_scale, wk, wv, q_scale, k_scale
             nc.sync.dma_start(out=dst[kind][m * P : (m + 1) * P, j * NT : (j + 1) * NT], in_=result[:].rearrange("p h c e -> p (h c e)"))
 
         def rotate(i):
-            inv_rms[i] = work.tile([P, TOKEN_TILES * HEADS], F32, name="inv_rms", bufs=2)
-            nc.vector.reciprocal(out=inv_rms[i][:], in_=rms[i][:])
             for m in range(TOKEN_TILES):
                 multiply_tables(i, m)
                 if m >= 1:
@@ -339,8 +329,8 @@ def tile_attention_pa_kernel(tc, x, wq_bytes, wq_scale, wk, wv, q_scale, k_scale
                     if max(u + 2, X_STEP + 1 + m) == s:
                         multiply(u, m)
             if s == CHAIN_STEPS - 1:
-                nc.scalar.activation(out=sines[:].rearrange("p a j i -> p (a j i)"), in_=rest[3][:], func=ACT.Sin)
-                nc.scalar.activation(out=unused[:], in_=freq[:, 0:1], func=ACT.Sqrt)
+                nc.scalar.activation(out=sines[:].rearrange("p a j i -> p (a j i)"), in_=rest[1][:], func=ACT.Sin)
+                nc.scalar.activation(out=unused[:], in_=freq[:, 0:1], func=ACT.Abs_reciprocal_sqrt)
             if s == X_READY + 1:
                 sum_squares(0)
             if i is not None:

@@ -37,15 +37,13 @@ NORMED_TILES = len(COLUMN_TILES) - 1
 FIRST_Q_UNIT = PASSES
 LAST_Q_UNIT = 5 * PASSES - 1
 
-WIDE_BUFS = 6
+WIDE_LEAD = 6
+WIDE_BUFS = 8
 SCALAR_UNITS = (18, 19, 20, 21, 22, 23)
 SCALAR_COPY_LEAD = 4
 X_STEP = 3
 X_READY = X_STEP + TOKEN_TILES
 ROTATE_LAG = 10
-CHAIN_HEAD = 12
-CHAIN_PER_STEP = 2
-CHAIN_STEPS = 2
 TABLE_STEP = 5
 
 
@@ -155,11 +153,6 @@ def tile_attention_pa_kernel(tc, x, wq_bytes, wq_scale, wk, wv, q_scale, k_scale
         chain.append(lambda: nc.vector.tensor_copy(out=turns[:], in_=turns_i[:]))
         chain.append(minus_turns(rest[0], turns, TWO_PI_HI, angle_flat))
         chain.append(minus_turns(rest[1], turns, TWO_PI_LO, rest[0][:]))
-        assert len(chain) == CHAIN_HEAD + CHAIN_PER_STEP * CHAIN_STEPS
-
-        def run_chain(first, last):
-            for link in chain[first:last]:
-                link()
 
         gains = const.tile([P, 2 * HD], F32, name="gains")
         gains_by_half = gains[:].rearrange("p (k c e) -> p k c e", k=2, c=2)
@@ -298,7 +291,8 @@ def tile_attention_pa_kernel(tc, x, wq_bytes, wq_scale, wk, wv, q_scale, k_scale
 
         gain_bank = psum.tile([P, 2 * HD], F32, name="bank3")
         nc.tensor.matmul(out=gain_bank[:], lhsT=ones[:], rhs=gain_rows[:], start=True, stop=True)
-        run_chain(0, CHAIN_HEAD)
+        for link in chain:
+            link()
         for u in range(FIRST_Q_UNIT, FIRST_Q_UNIT + PASSES):
             widen(u)
         add_waiting = []
@@ -312,8 +306,6 @@ def tile_attention_pa_kernel(tc, x, wq_bytes, wq_scale, wk, wv, q_scale, k_scale
                 nc.vector.tensor_copy(out=gains[:], in_=gain_bank[:])
             if s >= 1:
                 quantise(s - 1)
-            if s < CHAIN_STEPS:
-                run_chain(CHAIN_HEAD + CHAIN_PER_STEP * s, CHAIN_HEAD + CHAIN_PER_STEP * (s + 1))
             if X_STEP < s <= X_READY:
                 quantise_x(s - X_STEP - 1)
             if X_STEP <= s < X_READY:
@@ -328,15 +320,15 @@ def tile_attention_pa_kernel(tc, x, wq_bytes, wq_scale, wk, wv, q_scale, k_scale
                 for m in range(TOKEN_TILES):
                     if max(u + 2, X_STEP + 1 + m) == s:
                         multiply(u, m)
-            if s == CHAIN_STEPS - 1:
+            if s == 0:
                 nc.scalar.activation(out=sines[:].rearrange("p a j i -> p (a j i)"), in_=rest[1][:], func=ACT.Sin)
                 nc.scalar.activation(out=unused[:], in_=freq[:, 0:1], func=ACT.Abs_reciprocal_sqrt)
             if s == X_READY + 1:
                 sum_squares(0)
             if i is not None:
                 sum_squares(i + 1)
-            if 2 <= s and s + WIDE_BUFS <= LAST_Q_UNIT:
-                widen(s + WIDE_BUFS)
+            if 2 <= s and s + WIDE_LEAD <= LAST_Q_UNIT:
+                widen(s + WIDE_LEAD)
             if s + SCALAR_COPY_LEAD in SCALAR_UNITS:
                 interleave(s + SCALAR_COPY_LEAD)
         for m in range(TOKEN_TILES):

@@ -37,6 +37,7 @@ NORMED_TILES = len(COLUMN_TILES) - 1
 FIRST_Q_UNIT = PASSES
 LAST_Q_UNIT = 5 * PASSES - 1
 
+RUN = 8
 WIDE_LEAD = 6
 WIDE_BUFS = 8
 SCALAR_UNITS = (18, 19, 20, 21, 22, 23)
@@ -212,8 +213,8 @@ def tile_attention_pa_kernel(tc, x, wq_bytes, wq_scale, wk, wv, q_scale, k_scale
                 grouped[u] = work.tile([P, NT, PACK], BF16, name="grouped_by_scalar", bufs=len(SCALAR_UNITS), align_bytes=64)
             else:
                 grouped[u] = work.tile([P, NT, PACK], BF16, name="grouped", bufs=3, align_bytes=64)
-            out_view = grouped[u][:].rearrange("p (c i) t -> p c t i", i=4)
-            in_view = src[:].rearrange("p t (c i) -> p c t i", i=4)
+            out_view = grouped[u][:].rearrange("p (c i) t -> p c t i", i=RUN)
+            in_view = src[:].rearrange("p t (c i) -> p c t i", i=RUN)
             if on_scalar:
                 nc.scalar.copy(out=out_view, in_=in_view)
             else:

@@ -45,6 +45,7 @@ SCALAR_COPY_LEAD = 4
 X_STEP = 3
 X_READY = X_STEP + TOKEN_TILES
 ROTATE_LAG = 10
+PER_BANK = (4,)
 TABLE_STEP = 5
 
 
@@ -247,14 +248,19 @@ def tile_attention_pa_kernel(tc, x, wq_bytes, wq_scale, wk, wv, q_scale, k_scale
 
         def sum_squares(i):
             sums = work.tile([P, TOKEN_TILES * HEADS], F32, name="sums", bufs=2)
+            if i in PER_BANK:
+                inv_rms[i] = work.tile([P, TOKEN_TILES * HEADS], F32, name="inv_rms", bufs=2)
             for m in range(TOKEN_TILES):
                 for h in range(HEADS):
                     squares = work.tile([P, HD], BF16, name="squares", bufs=2)
                     nc.scalar.activation(
                         out=squares[:], in_=acc[(i, m)][:, h * HD : (h + 1) * HD], func=ACT.Square, accum_out=sums[:, m * HEADS + h : m * HEADS + h + 1]
                     )
-            inv_rms[i] = work.tile([P, TOKEN_TILES * HEADS], F32, name="inv_rms", bufs=2)
-            nc.scalar.activation(out=inv_rms[i][:], in_=sums[:], func=ACT.Abs_reciprocal_sqrt, bias=EPS, scale=1.0 / HD)
+                if i in PER_BANK:
+                    nc.scalar.activation(out=inv_rms[i][:, m * HEADS : (m + 1) * HEADS], in_=sums[:, m * HEADS : (m + 1) * HEADS], func=ACT.Abs_reciprocal_sqrt, bias=EPS, scale=1.0 / HD)
+            if i not in PER_BANK:
+                inv_rms[i] = work.tile([P, TOKEN_TILES * HEADS], F32, name="inv_rms", bufs=2)
+                nc.scalar.activation(out=inv_rms[i][:], in_=sums[:], func=ACT.Abs_reciprocal_sqrt, bias=EPS, scale=1.0 / HD)
 
         def multiply_tables(i, m):
             kind = COLUMN_TILES[i][0]

from contextlib import ExitStack

import concourse.mybir as mybir
from concourse.masks import make_identity

F32 = mybir.dt.float32
BF16 = mybir.dt.bfloat16
U32 = mybir.dt.uint32
I32 = mybir.dt.int32
U8 = mybir.dt.uint8
FP8 = mybir.dt.float8_e4m3fn
FP8X4 = mybir.dt.float8_e4m3fn_x4
ACT = mybir.ActivationFunctionType
ALU = mybir.AluOpType

P = 128
PACK = 4
DM = 2048
PASSES = DM // (P * PACK)
TOKENS = 512
TOKEN_TILES = TOKENS // P
NT = 512
HD = 128
HALF = HD // 2
HEADS = NT // HD
THETA = 10000.0
EPS = 1e-6
PI = 3.141592653589793
TWO_PI_HI = 6.28125
TWO_PI_LO = 2.0 * PI - TWO_PI_HI

FLOPS = 2 * TOKENS * DM * (2048 + 512 + 512)

COLUMN_TILES = (("k", 0), ("q", 0), ("q", 1), ("q", 2), ("q", 3), ("v", 0))
UNITS = len(COLUMN_TILES) * PASSES
NORMED_TILES = len(COLUMN_TILES) - 1
FIRST_Q_UNIT = PASSES
LAST_Q_UNIT = 5 * PASSES - 1

RUN = 8
WIDE_LEAD = 6
WIDE_BUFS = 8
SCALAR_UNITS = (18, 19, 20, 21, 22, 23)
SCALAR_COPY_LEAD = 4
X_STEP = 3
X_READY = X_STEP + TOKEN_TILES
ROTATE_LAG = 10
PER_BANK = (4,)
TABLE_STEP = 5


def rotated_in(step):
    i, beyond = divmod(step - ROTATE_LAG, PASSES)
    return i if (beyond == 0 and 0 <= i < NORMED_TILES - 1) else None


def tile_attention_pa_kernel(tc, x, wq_bytes, wq_scale, wk, wv, q_scale, k_scale, out_0, out_1, out_2):
    nc = tc.nc
    x_flat = x.flatten_outer_dims()
    wq_bytes_v = wq_bytes.rearrange("(g p t) h d -> g p t (h d)", p=P, t=PACK)
    wq_scale_v = wq_scale.rearrange("(g p t) a b -> p g (t a b)", p=P, t=PACK)
    w_v = {
        "k": wk.rearrange("(g p t) h d -> g p t (h d)", p=P, t=PACK),
        "v": wv.rearrange("(g p t) h d -> g p t (h d)", p=P, t=PACK),
    }
    dst = {
        "q": out_0.rearrange("b s h d -> (b s) (h d)"),
        "k": out_1.rearrange("b s h d -> (b s) (h d)"),
        "v": out_2.rearrange("b s h d -> (b s) (h d)"),
    }

    with ExitStack() as ctx:
        const = ctx.enter_context(tc.tile_pool(name="const", bufs=1))
        raw = ctx.enter_context(tc.tile_pool(name="raw", bufs=1))
        keep = ctx.enter_context(tc.tile_pool(name="keep", bufs=1))
        work = ctx.enter_context(tc.tile_pool(name="work", bufs=2))
        psum = ctx.enter_context(tc.psum_pool(name="psum", bufs=1))
        ctx.enter_context(tc.manual_schedule())

        scales = const.tile([P, PASSES, PACK], F32, name="wq_scales")
        gain_rows = const.tile([P, 2 * HD], BF16, name="gain_rows")
        nc.vector.memset(gain_rows[:], 0.0)
        x_raw = [raw.tile([P, DM], BF16, name="x_raw%d" % m) for m in range(TOKEN_TILES)]
        wq_raw = {}
        w_raw = {}

        def load_wq(j, g, cuts=(0, PACK)):
            wq_raw[(j, g)] = raw.tile([P, PACK, NT], U8, name="wq_bytes_%d_%d" % (j, g))
            for t0, t1 in zip(cuts[:-1], cuts[1:]):
                nc.sync.dma_start(out=wq_raw[(j, g)][:, t0:t1, :], in_=wq_bytes_v[g][:, t0:t1, j * NT : (j + 1) * NT])

        def load_w(kind, g):
            w_raw[(kind, g)] = raw.tile([P, PACK, NT], BF16, name="w%s_raw%d" % (kind, g))
            nc.sync.dma_start(out=w_raw[(kind, g)][:], in_=w_v[kind][g])

        nc.sync.dma_start(out=scales[:], in_=wq_scale_v)
        load_wq(0, 0, cuts=(0, 1, PACK))
        nc.sync.dma_start(out=gain_rows[0:1, 0:HD], in_=q_scale.unsqueeze(0))
        nc.sync.dma_start(out=gain_rows[0:1, HD : 2 * HD], in_=k_scale.unsqueeze(0))
        for g in range(PASSES):
            load_w("k", g)
            if g + 1 < PASSES:
                load_wq(0, g + 1)
        for m in range(TOKEN_TILES):
            nc.sync.dma_start(out=x_raw[m][:], in_=x_flat[m * P : (m + 1) * P, :])
            load_wq(1, m)
        for g in range(PASSES):
            load_wq(2, g)
        for g in range(PASSES):
            load_w("v", g)
            load_wq(3, g)

        ident = const.tile([P, P], F32, name="ident")
        make_identity(nc, ident[:])
        ones = const.tile([P, P], BF16, name="ones")
        nc.vector.memset(ones[:], 1.0)
        zero = const.tile([P, 1], F32, name="zero")
        nc.vector.memset(zero[:], 0.0)
        unused = const.tile([P, 1], F32, name="unused")
        nc.scalar.activation(out=unused[:], in_=zero[:], func=ACT.Sin)

        position_i = const.tile([P, 2], I32, name="position_i")
        nc.gpsimd.iota(position_i[:], pattern=[[P, 2]], base=0, channel_multiplier=1)
        position = const.tile([P, 2], F32, name="position")
        freq = const.tile([P, HALF], F32, name="freq")
        angle = const.tile([P, 2, 2, HALF], F32, name="angle")
        angle_flat = angle[:].rearrange("p a j i -> p (a j i)")
        turns_i = const.tile([P, 4 * HALF], I32, name="turns_i")
        turns = const.tile([P, 4 * HALF], F32, name="turns")
        rest = [const.tile([P, 4 * HALF], F32, name="rest%d" % n) for n in range(2)]
        sines = const.tile([P, 2, 2, HALF], F32, name="sines")

        def minus_turns(out, count, part, from_):
            return lambda: nc.vector.scalar_tensor_tensor(out=out[:], in0=count[:], scalar=-part, in1=from_, op0=ALU.mult, op1=ALU.add)

        chain = []
        chain.append(lambda: nc.vector.memset(freq[:, 0:1], 1.0))
        chain.append(lambda: nc.vector.tensor_copy(out=position[:], in_=position_i[:]))
        for b in range(6):
            chain.append(
                lambda w=(1 << b): nc.vector.tensor_scalar(
                    out=freq[:, w : 2 * w], in0=freq[:, 0:w], scalar1=pow(THETA, -w / 64.0), scalar2=None, op0=ALU.mult
                )
            )
        for j in range(2):
            chain.append(
                lambda j=j: nc.vector.tensor_scalar(out=angle[:, 0, j, :], in0=freq[:], scalar1=position[:, j : j + 1], scalar2=None, op0=ALU.mult)
            )
            chain.append(
                lambda j=j: nc.vector.tensor_scalar(
                    out=angle[:, 1, j, :], in0=freq[:], scalar1=position[:, j : j + 1], scalar2=PI / 2.0, op0=ALU.mult, op1=ALU.add
                )
            )
        chain.append(lambda: nc.vector.tensor_scalar(out=turns_i[:], in0=angle_flat, scalar1=1.0 / (2.0 * PI), scalar2=None, op0=ALU.mult))
        chain.append(lambda: nc.vector.tensor_copy(out=turns[:], in_=turns_i[:]))
        chain.append(minus_turns(rest[0], turns, TWO_PI_HI, angle_flat))
        chain.append(minus_turns(rest[1], turns, TWO_PI_LO, rest[0][:]))

        gains = const.tile([P, 2 * HD], F32, name="gains")
        gains_by_half = gains[:].rearrange("p (k c e) -> p k c e", k=2, c=2)
        KIND_INDEX = {"q": 0, "k": 1}
        tables = const.tile([P, 2, 2, 2, 2, HALF], F32, name="tables")

        def build_tables():
            for j in range(2):
                sin_j = sines[:, 0, j, :]
                cos_j = sines[:, 1, j, :]
                nc.vector.tensor_tensor(
                    out=tables[:, :, j, 0, :, :], in0=gains_by_half, in1=cos_j.unsqueeze(1).unsqueeze(1).to_broadcast([P, 2, 2, HALF]), op=ALU.mult
                )
                sin_both = sin_j.unsqueeze(1).to_broadcast([P, 2, HALF])
                nc.vector.tensor_tensor(out=tables[:, :, j, 1, 0, :], in0=gains_by_half[:, :, 0, :], in1=sin_both, op=ALU.mult)
                nc.vector.scalar_tensor_tensor(
                    out=tables[:, :, j, 1, 1, :], in0=gains_by_half[:, :, 1, :], scalar=-1.0, in1=sin_both, op0=ALU.mult, op1=ALU.mult
                )

        x_codes = [keep.tile([P, PASSES * P], U32, name="x_codes%d" % m, align_bytes=64) for m in range(TOKEN_TILES)]
        x_scales = [keep.tile([P, PASSES * P], U8, name="x_scales%d" % m, align_bytes=64) for m in range(TOKEN_TILES)]
        x_grouped = {}

        def turn_x(m):
            words = x_raw[m][:].bitcast(F32)
            x_grouped[m] = work.tile([P, PASSES, P, PACK], BF16, name="x_grouped", bufs=2, align_bytes=64)
            grouped_words = x_grouped[m][:].rearrange("p g r t -> p (g r t)").bitcast(F32).rearrange("p (g r u) -> p g r u", g=PASSES, u=2)
            for half in range(2):
                bank = psum.tile([P, 2, 2, P], F32, name="bank%d" % (4 + 2 * (m % 2) + half))
                for g2 in range(2):
                    g = 2 * half + g2
                    for u in range(2):
                        nc.tensor.transpose(bank[:, g2, u, :], words[:, 256 * g + u : 256 * (g + 1) : 2], ident[:])
                src = bank[:].rearrange("p g u r -> p g r u")
                nc.vector.tensor_copy(out=grouped_words[:, 2 * half : 2 * half + 2], in_=src)

        def quantise_x(m):
            nc.vector.quantize_mx(out=x_codes[m][:].bitcast(FP8X4), scales=x_scales[m][:], in_=x_grouped[m][:].rearrange("p g r t -> p (g r t)"))

        wide = {}
        grouped = {}
        w_codes = {}
        w_scales = {}

        def widen(u):
            j = COLUMN_TILES[u // PASSES][1]
            g = u % PASSES
            wide[u] = work.tile([P, PACK, NT], BF16, name="wide", bufs=WIDE_BUFS)
            for t in range(PACK):
                nc.scalar.activation(out=wide[u][:, t, :], in_=wq_raw[(j, g)][:, t, :].bitcast(FP8), func=ACT.Copy, scale=scales[:, g, t : t + 1])

        def interleave(u):
            kind = COLUMN_TILES[u // PASSES][0]
            src = wide[u] if kind == "q" else w_raw[(kind, u % PASSES)]
            on_scalar = u in SCALAR_UNITS
            if on_scalar:
                grouped[u] = work.tile([P, NT, PACK], BF16, name="grouped_by_scalar", bufs=len(SCALAR_UNITS), align_bytes=64)
            else:
                grouped[u] = work.tile([P, NT, PACK], BF16, name="grouped", bufs=3, align_bytes=64)
            out_view = grouped[u][:].rearrange("p (c i) t -> p c t i", i=RUN)
            in_view = src[:].rearrange("p t (c i) -> p c t i", i=RUN)
            if on_scalar:
                nc.scalar.copy(out=out_view, in_=in_view)
            else:
                nc.vector.tensor_copy(out=out_view, in_=in_view)

        def quantise(u):
            w_codes[u] = work.tile([P, NT], U32, name="w_codes", bufs=8, align_bytes=64)
            w_scales[u] = work.tile([P, NT], U8, name="w_scales", bufs=8, align_bytes=64)
            nc.vector.quantize_mx(out=w_codes[u][:].bitcast(FP8X4), scales=w_scales[u][:], in_=grouped[u][:].rearrange("p n t -> p (n t)"))

        acc = {}

        def multiply(u, m):
            i = u // PASSES
            g = u % PASSES
            if g == 0:
                acc[(i, m)] = psum.tile([P, NT], F32, name="bank%d" % (TOKEN_TILES * (i % 2) + m))
            nc.tensor.matmul_mx(
                out=acc[(i, m)][:],
                lhsT=x_codes[m][:, g * P : (g + 1) * P].bitcast(FP8X4),
                lhsT_scale=x_scales[m][:, g * P : (g + 1) * P],
                rhs=w_codes[u][:].bitcast(FP8X4),
                rhs_scale=w_scales[u][:],
                start=(g == 0),
                stop=(g == PASSES - 1),
            )

        inv_rms = {}
        products = {}

        def sum_squares(i):
            sums = work.tile([P, TOKEN_TILES * HEADS], F32, name="sums", bufs=2)
            if i in PER_BANK:
                inv_rms[i] = work.tile([P, TOKEN_TILES * HEADS], F32, name="inv_rms", bufs=2)
            for m in range(TOKEN_TILES):
                for h in range(HEADS):
                    squares = work.tile([P, HD], BF16, name="squares", bufs=2)
                    nc.scalar.activation(
                        out=squares[:], in_=acc[(i, m)][:, h * HD : (h + 1) * HD], func=ACT.Square, accum_out=sums[:, m * HEADS + h : m * HEADS + h + 1]
                    )
                if i in PER_BANK:
                    nc.scalar.activation(out=inv_rms[i][:, m * HEADS : (m + 1) * HEADS], in_=sums[:, m * HEADS : (m + 1) * HEADS], func=ACT.Abs_reciprocal_sqrt, bias=EPS, scale=1.0 / HD)
            if i not in PER_BANK:
                inv_rms[i] = work.tile([P, TOKEN_TILES * HEADS], F32, name="inv_rms", bufs=2)
                nc.scalar.activation(out=inv_rms[i][:], in_=sums[:], func=ACT.Abs_reciprocal_sqrt, bias=EPS, scale=1.0 / HD)

        def multiply_tables(i, m):
            kind = COLUMN_TILES[i][0]
            table = tables[:, KIND_INDEX[kind], m % 2, :, :, :].rearrange("p w c e -> p w (c e)")
            products[(i, m)] = work.tile([P, HEADS, 2, 2, HALF], F32, name="products", bufs=4)
            for h in range(HEADS):
                nc.vector.scalar_tensor_tensor(
                    out=products[(i, m)][:, h, :, :, :].rearrange("p w c e -> p w (c e)"),
                    in0=acc[(i, m)][:, h * HD : (h + 1) * HD].unsqueeze(1).to_broadcast([P, 2, HD]),
                    scalar=inv_rms[i][:, m * HEADS + h : m * HEADS + h + 1],
                    in1=table,
                    op0=ALU.mult,
                    op1=ALU.mult,
                )

        def add_products(i, m, engine, ring, bufs):
            kind, j = COLUMN_TILES[i]
            result = work.tile([P, HEADS, 2, HALF], F32, name=ring, bufs=bufs)
            engine.tensor_tensor(out=result[:], in0=products[(i, m)][:, :, 0, :, :], in1=products[(i, m)][:, :, 1, ::-1, :], op=ALU.add)
            nc.sync.dma_start(out=dst[kind][m * P : (m + 1) * P, j * NT : (j + 1) * NT], in_=result[:].rearrange("p h c e -> p (h c e)"))

        def rotate(i):
            for m in range(TOKEN_TILES):
                multiply_tables(i, m)
                if m >= 1:
                    add_products(i, m - 1, nc.gpsimd, "result_by_gpsimd", 4)

        def add_last(i):
            add_products(i, TOKEN_TILES - 1, nc.vector, "result_by_vector", 2)

        def store_v(m):
            v_result = work.tile([P, NT], F32, name="v_result", bufs=4)
            nc.scalar.copy(out=v_result[:], in_=acc[(len(COLUMN_TILES) - 1, m)][:])
            nc.sync.dma_start(out=dst["v"][m * P : (m + 1) * P, :], in_=v_result[:])

        gain_bank = psum.tile([P, 2 * HD], F32, name="bank3")
        nc.tensor.matmul(out=gain_bank[:], lhsT=ones[:], rhs=gain_rows[:], start=True, stop=True)
        for link in chain:
            link()
        for u in range(FIRST_Q_UNIT, FIRST_Q_UNIT + PASSES):
            widen(u)
        add_waiting = []
        for s in range(UNITS + 1):
            if s < UNITS and s not in SCALAR_UNITS:
                interleave(s)
            for i in add_waiting:
                add_last(i)
            add_waiting = []
            if s == 0:
                nc.vector.tensor_copy(out=gains[:], in_=gain_bank[:])
            if s >= 1:
                quantise(s - 1)
            if X_STEP < s <= X_READY:
                quantise_x(s - X_STEP - 1)
            if X_STEP <= s < X_READY:
                turn_x(s - X_STEP)
            if s == TABLE_STEP:
                build_tables()
            i = rotated_in(s)
            if i is not None:
                rotate(i)
                add_waiting.append(i)
            for u in range(s - 1):
                for m in range(TOKEN_TILES):
                    if max(u + 2, X_STEP + 1 + m) == s:
                        multiply(u, m)
            if s == 0:
                nc.scalar.activation(out=sines[:].rearrange("p a j i -> p (a j i)"), in_=rest[1][:], func=ACT.Sin)
                nc.scalar.activation(out=unused[:], in_=freq[:, 0:1], func=ACT.Abs_reciprocal_sqrt)
            if s == X_READY + 1:
                sum_squares(0)
            if i is not None:
                sum_squares(i + 1)
            if 2 <= s and s + WIDE_LEAD <= LAST_Q_UNIT:
                widen(s + WIDE_LEAD)
            if s + SCALAR_COPY_LEAD in SCALAR_UNITS:
                interleave(s + SCALAR_COPY_LEAD)
        for m in range(TOKEN_TILES):
            multiply(UNITS - 1, m)
        for m in range(TOKEN_TILES):
            store_v(m)
        rotate(NORMED_TILES - 1)
        add_last(NORMED_TILES - 1)
